import numpy as np
import ml_dtypes


def mxq(x, axis, fmt="e4m3"):
    dtype, down = {"e4m3": (ml_dtypes.float8_e4m3fn, 7), "e5m2": (ml_dtypes.float8_e5m2, 14)}[fmt]
    v = np.moveaxis(np.asarray(x, np.float32).astype(ml_dtypes.bfloat16).astype(np.float64), axis, -1)
    blocks = v.reshape(v.shape[:-1] + (-1, 32))
    amax = np.abs(blocks).max(-1, keepdims=True)
    byte = np.maximum(np.where(amax > 0, np.frexp(amax)[1] - 1 + 127, 0) - down, 1)
    scale = np.exp2(byte - 127.0)
    codes = (blocks / scale).astype(np.float32).astype(dtype).astype(np.float64)
    return np.moveaxis((codes * scale).reshape(v.shape), -1, axis)


WIDE = False


def mx_kscale(k):
    if not WIDE:
        return np.ones(k)
    levels = np.array([10, -10, 5, -5, 0])
    a = np.random.permutation(np.resize(levels, k // 512 * 4)).reshape(k // 512, 4)
    idx = np.arange(k)
    return np.exp2(a[idx // 512, idx % 128 // 32])


BF16 = ml_dtypes.bfloat16


def bf(x):
    return np.asarray(x, np.float32).astype(BF16)


def f64(x):
    return np.asarray(x).astype(np.float64)


B, H, S, D, BLOCK_SIZE, NUM_BLOCKS = 1, 4, 4096, 128, 512, 3


def setup_inputs():
    t = mx_kscale(S)
    q = np.random.standard_normal((B, H, S, D)) * 1.5
    k = np.random.standard_normal((B, H, S, D))
    v = np.random.standard_normal((B, H, S, D)) * 4.0
    q[..., 0] = 8.0
    k[..., 0] += np.log(t) * np.sqrt(D) / 8.0
    v *= (t.mean() / t)[:, None]
    return {"q": bf(q), "k": bf(k), "v": bf(v)}


def reference(q, k, v):
    q, k = f64(q), f64(k)
    scale = 1.0 / np.sqrt(D)
    vq = mxq(f64(v), 2, "e4m3")
    half = NUM_BLOCKS // 2
    nblk = S // BLOCK_SIZE
    out = []
    for i in range(nblk):
        lo = max(i - half, 0) * BLOCK_SIZE
        hi = min(i + half + 1, nblk) * BLOCK_SIZE
        qi = q[:, :, i * BLOCK_SIZE:(i + 1) * BLOCK_SIZE]
        s = qi @ k[:, :, lo:hi].transpose(0, 1, 3, 2) * scale
        e = np.exp(s - s.max(-1, keepdims=True))
        out.append((mxq(e, 3, "e4m3") @ vq[:, :, lo:hi]) / e.sum(-1, keepdims=True))
    return np.concatenate(out, 2)

@@ -1,0 +1,217 @@
+from contextlib import ExitStack
+import math
+
+import concourse.mybir as mybir
+from concourse.masks import make_identity
+
+F32 = mybir.dt.float32
+BF16 = mybir.dt.bfloat16
+U32 = mybir.dt.uint32
+U8 = mybir.dt.uint8
+FP8X4 = mybir.dt.float8_e4m3fn_x4
+ALU = mybir.AluOpType
+ACT = mybir.ActivationFunctionType
+AX = mybir.AxisListType
+
+H = 4
+S = 4096
+D = 128
+P = 128
+BLK = 512
+NBLK = S // BLK
+PACK = 4
+PAIRS = H * (3 * NBLK - 2)
+FLOPS = 2 * 2 * PAIRS * BLK * BLK * D
+SCALE = 1.0 / math.sqrt(D)
+
+VEC_OF = 3
+X_MODE = "P1"
+
+
+def tile_blocksparseattention_t_kernel(tc, q, k, v, out):
+    nc = tc.nc
+    with ExitStack() as ctx:
+        const = ctx.enter_context(tc.tile_pool(name="const", bufs=1))
+        raw = ctx.enter_context(tc.tile_pool(name="raw", bufs=3))
+        heads = ctx.enter_context(tc.tile_pool(name="heads", bufs=2))
+        work = ctx.enter_context(tc.tile_pool(name="work", bufs=3))
+        small = ctx.enter_context(tc.tile_pool(name="small", bufs=4))
+        ps_s = ctx.enter_context(tc.psum_pool(name="ps_s", bufs=3))
+        ps_t = ctx.enter_context(tc.psum_pool(name="ps_t", bufs=4))
+        ps_o = ctx.enter_context(tc.psum_pool(name="ps_o", bufs=1))
+
+        ident = const.tile([P, P], BF16, name="ident")
+        make_identity(nc, ident[:])
+
+        state = {"copies": 0}
+        raws = {}
+        kqs = {}
+        vcs = {}
+        vss = {}
+
+        def load(pair):
+            h, b2 = divmod(pair, NBLK // 2)
+            rows = slice(b2 * 2 * BLK, (b2 + 1) * 2 * BLK)
+            got = []
+            for nm, src in (("kraw", k), ("qraw", q), ("vraw", v)):
+                t = raw.tile([P, 2, BLK], BF16, name=nm, tag=nm)
+                nc.sync.dma_start(
+                    out=t[:],
+                    in_=src[0, h, rows, :].rearrange("(b p t) d -> p b (t d)", b=2, p=P, t=PACK),
+                )
+                got.append(t)
+            raws[pair] = got
+
+        def copy_out(dst, src):
+            n = state["copies"]
+            state["copies"] = n + 1
+            if n % VEC_OF == VEC_OF - 1:
+                nc.vector.tensor_copy(out=dst, in_=src)
+            else:
+                nc.scalar.copy(out=dst, in_=src)
+
+        def prep(g):
+            h, b = divmod(g, NBLK)
+            if b == 0:
+                kqs[h] = heads.tile([P, NBLK, 2 * BLK], BF16, name="kq", tag="kq")
+                vcs[h] = heads.tile([P, NBLK * D], U32, name="vcodes", tag="vcodes", align_bytes=64)
+                vss[h] = heads.tile([P, NBLK * D], U8, name="vscales", tag="vscales", align_bytes=64)
+            kraw, qraw, vraw = raws[g // 2]
+            tp = ps_t.tile([P, 2 * BLK], BF16, name="tp", tag="tp")
+            for x, src in enumerate((kraw, qraw)):
+                for t in range(PACK):
+                    nc.tensor.transpose(
+                        out=tp[:, x * BLK + t * P:x * BLK + (t + 1) * P],
+                        in_=src[:, b % 2, t * D:(t + 1) * D],
+                        identity=ident[:],
+                    )
+            nc.scalar.copy(out=kqs[h][:, b, :], in_=tp[:])
+            vg = work.tile([P, BLK], BF16, name="vg", tag="vg", align_bytes=64)
+            nc.vector.tensor_copy(
+                out=vg[:].rearrange("p (d t) -> p d t", t=PACK),
+                in_=vraw[:, b % 2, :].rearrange("p (t d) -> p d t", t=PACK),
+            )
+            nc.vector.quantize_mx(
+                out=vcs[h][:, b * D:(b + 1) * D].bitcast(FP8X4),
+                scales=vss[h][:, b * D:(b + 1) * D],
+                in_=vg[:],
+            )
+
+        def main(g):
+            h, i = divmod(g, NBLK)
+            lo = max(i - 1, 0)
+            ncb = min(i + 2, NBLK) - lo
+            kq = kqs[h]
+            units = PACK * ncb
+            codes = work.tile([P, PACK * 3 * P], U32, name="codes", tag="codes", align_bytes=64)
+            scl = work.tile([P, PACK * 3 * P], U8, name="scl", tag="scl", align_bytes=64)
+            rs = small.tile([P, PACK * 3], F32, name="rs", tag="rs")
+            tp = None
+            for qt in range(PACK):
+                mx = small.tile([P, 4], F32, name="mx", tag="mx")
+                ssb = work.tile([P, 3 * BLK], F32, name="ssb", tag="ssb")
+                for c in range(ncb):
+                    sp = ps_s.tile([P, BLK], F32, name="sp", tag="sp")
+                    nc.tensor.matmul(
+                        out=sp[:],
+                        lhsT=kq[:, i, BLK + qt * P:BLK + (qt + 1) * P],
+                        rhs=kq[:, lo + c, 0:BLK],
+                        start=True,
+                        stop=True,
+                    )
+                    nc.vector.tensor_scalar(
+                        out=ssb[:, c * BLK:(c + 1) * BLK], in0=sp[:], scalar1=-SCALE, scalar2=None,
+                        op0=ALU.mult, op1=ALU.min, accum_out=mx[:, c:c + 1],
+                    )
+                negm = small.tile([P, 1], F32, name="negm", tag="negm")
+                if ncb == 2:
+                    nc.vector.tensor_scalar(
+                        out=negm[:], in0=mx[:, 0:1], scalar1=mx[:, 1:2], scalar2=None, op0=ALU.min,
+                    )
+                else:
+                    nc.vector.tensor_scalar(
+                        out=negm[:], in0=mx[:, 0:1], scalar1=mx[:, 1:2], scalar2=mx[:, 2:3],
+                        op0=ALU.min, op1=ALU.min,
+                    )
+                e = work.tile([P, 3 * BLK], BF16, name="e", tag="e")
+                for c in range(ncb):
+                    u = qt * ncb + c
+                    nc.scalar.activation(
+                        out=e[:, c * BLK:(c + 1) * BLK], in_=ssb[:, c * BLK:(c + 1) * BLK], func=ACT.Exp,
+                        bias=negm[:, 0:1], scale=-1.0, accum_out=rs[:, u:u + 1],
+                    )
+                for c in range(ncb):
+                    u = qt * ncb + c
+                    if u % 2 == 0:
+                        tp = ps_t.tile([P, 2 * BLK], BF16, name="tp", tag="tp")
+                    for t in range(PACK):
+                        nc.tensor.transpose(
+                            out=tp[:, (u % 2) * BLK + t * P:(u % 2) * BLK + (t + 1) * P],
+                            in_=e[:, c * BLK + t * P:c * BLK + (t + 1) * P],
+                            identity=ident[:],
+                        )
+                    if u % 2 == 1:
+                        grp = work.tile([P, 2 * BLK], BF16, name="grp", tag="grp", align_bytes=64)
+                        if X_MODE == "P1":
+                            copy_out(
+                                grp[:].rearrange("p (u q t) -> p u q t", u=2, t=PACK),
+                                tp[:].rearrange("p (u t q) -> p u q t", u=2, t=PACK),
+                            )
+                        else:
+                            pln = work.tile([P, 2 * BLK], BF16, name="pln", tag="pln")
+                            nc.scalar.copy(out=pln[:], in_=tp[:])
+                            nc.gpsimd.tensor_scalar(
+                                out=grp[:].rearrange("p (u q t) -> p u q t", u=2, t=PACK),
+                                in0=pln[:].rearrange("p (u t q) -> p u q t", u=2, t=PACK),
+                                scalar1=1.0, scalar2=0.0, op0=ALU.mult, op1=ALU.add,
+                            )
+                        w0 = (u - 1) * P
+                        nc.vector.quantize_mx(
+                            out=codes[:, w0:w0 + 2 * P].bitcast(FP8X4),
+                            scales=scl[:, w0:w0 + 2 * P],
+                            in_=grp[:],
+                        )
+            pv = ps_o.tile([P, PACK * D], F32, name="pv", tag="pv")
+            for qt in range(PACK):
+                for c in range(ncb):
+                    u = qt * ncb + c
+                    nc.tensor.matmul_mx(
+                        out=pv[:, qt * D:(qt + 1) * D],
+                        lhsT=codes[:, u * P:(u + 1) * P].bitcast(FP8X4),
+                        lhsT_scale=scl[:, u * P:(u + 1) * P],
+                        rhs=vcs[h][:, (lo + c) * D:(lo + c + 1) * D].bitcast(FP8X4),
+                        rhs_scale=vss[h][:, (lo + c) * D:(lo + c + 1) * D],
+                        start=(c == 0),
+                        stop=(c == ncb - 1),
+                    )
+            rsum = small.tile([P, PACK], F32, name="rsum", tag="rsum")
+            nc.vector.tensor_reduce(
+                out=rsum[:], in_=rs[:, 0:units].rearrange("p (a c) -> p a c", c=ncb),
+                axis=AX.X, op=ALU.add,
+            )
+            rinv = small.tile([P, PACK], F32, name="rinv", tag="rinv")
+            nc.vector.reciprocal(out=rinv[:], in_=rsum[:])
+            o_sb = work.tile([P, PACK * D], F32, name="o_sb", tag="o_sb")
+            nc.vector.tensor_tensor(
+                out=o_sb[:].rearrange("p (a d) -> p a d", a=PACK),
+                in0=pv[:].rearrange("p (a d) -> p a d", a=PACK),
+                in1=rinv[:].unsqueeze(2).to_broadcast([P, PACK, D]),
+                op=ALU.mult,
+            )
+            nc.sync.dma_start(
+                out=out[0, h, i * BLK:(i + 1) * BLK, :].rearrange("(p t) d -> p (t d)", t=PACK),
+                in_=o_sb[:],
+            )
+
+        total = H * NBLK
+        load(0)
+        load(1)
+        prep(0)
+        prep(1)
+        for g in range(total):
+            nxt = g + 2
+            if nxt < total:
+                if nxt % 2 == 0 and nxt // 2 + 1 < total // 2:
+                    load(nxt // 2 + 1)
+                prep(nxt)
+            main(g)

@@ -25,7 +25,7 @@ FLOPS = 2 * 2 * PAIRS * BLK * BLK * D
 SCALE = 1.0 / math.sqrt(D)
 
 VEC_OF = 3
-X_MODE = "P1"
+X_MODE = "G"
 
 
 def tile_blocksparseattention_t_kernel(tc, q, k, v, out):
@@ -34,7 +34,7 @@ def tile_blocksparseattention_t_kernel(tc, q, k, v, out):
         const = ctx.enter_context(tc.tile_pool(name="const", bufs=1))
         raw = ctx.enter_context(tc.tile_pool(name="raw", bufs=3))
         heads = ctx.enter_context(tc.tile_pool(name="heads", bufs=2))
-        work = ctx.enter_context(tc.tile_pool(name="work", bufs=3))
+        work = ctx.enter_context(tc.tile_pool(name="work", bufs=4))
         small = ctx.enter_context(tc.tile_pool(name="small", bufs=4))
         ps_s = ctx.enter_context(tc.psum_pool(name="ps_s", bufs=3))
         ps_t = ctx.enter_context(tc.psum_pool(name="ps_t", bufs=4))
@@ -87,9 +87,10 @@ def tile_blocksparseattention_t_kernel(tc, q, k, v, out):
                     )
             nc.scalar.copy(out=kqs[h][:, b, :], in_=tp[:])
             vg = work.tile([P, BLK], BF16, name="vg", tag="vg", align_bytes=64)
-            nc.vector.tensor_copy(
+            nc.gpsimd.tensor_scalar(
                 out=vg[:].rearrange("p (d t) -> p d t", t=PACK),
-                in_=vraw[:, b % 2, :].rearrange("p (t d) -> p d t", t=PACK),
+                in0=vraw[:, b % 2, :].rearrange("p (t d) -> p d t", t=PACK),
+                scalar1=1.0, scalar2=0.0, op0=ALU.mult, op1=ALU.add,
             )
             nc.vector.quantize_mx(
                 out=vcs[h][:, b * D:(b + 1) * D].bitcast(FP8X4),

@@ -24,8 +24,11 @@ PAIRS = H * (3 * NBLK - 2)
 FLOPS = 2 * 2 * PAIRS * BLK * BLK * D
 SCALE = 1.0 / math.sqrt(D)
 
-VEC_OF = 3
-X_MODE = "G"
+VEC_OF = 0
+PINNED = True
+GRP = 4
+QG = P // GRP
+LAG = 8
 
 
 def tile_blocksparseattention_t_kernel(tc, q, k, v, out):
@@ -34,7 +37,7 @@ def tile_blocksparseattention_t_kernel(tc, q, k, v, out):
         const = ctx.enter_context(tc.tile_pool(name="const", bufs=1))
         raw = ctx.enter_context(tc.tile_pool(name="raw", bufs=3))
         heads = ctx.enter_context(tc.tile_pool(name="heads", bufs=2))
-        work = ctx.enter_context(tc.tile_pool(name="work", bufs=4))
+        work = ctx.enter_context(tc.tile_pool(name="work", bufs=3))
         small = ctx.enter_context(tc.tile_pool(name="small", bufs=4))
         ps_s = ctx.enter_context(tc.psum_pool(name="ps_s", bufs=3))
         ps_t = ctx.enter_context(tc.psum_pool(name="ps_t", bufs=4))
@@ -43,11 +46,30 @@ def tile_blocksparseattention_t_kernel(tc, q, k, v, out):
         ident = const.tile([P, P], BF16, name="ident")
         make_identity(nc, ident[:])
 
-        state = {"copies": 0}
+        perm = const.tile([P, P], BF16, name="perm")
+        nc.vector.tensor_copy(
+            out=perm[:].rearrange("p (q g) -> p q g", g=GRP),
+            in_=ident[:].rearrange("p (g q) -> p q g", g=GRP),
+        )
+
+        if PINNED:
+            ctx.enter_context(tc.manual_schedule())
+
+        total = H * NBLK
+        ntiles = total * PACK
         raws = {}
         kqs = {}
         vcs = {}
         vss = {}
+        preps = {}
+        blocks = {}
+        tiles = {}
+        state = {"copies": 0, "tp": None}
+
+        def span(g):
+            i = g % NBLK
+            lo = max(i - 1, 0)
+            return lo, min(i + 2, NBLK) - lo
 
         def load(pair):
             h, b2 = divmod(pair, NBLK // 2)
@@ -62,15 +84,7 @@ def tile_blocksparseattention_t_kernel(tc, q, k, v, out):
                 got.append(t)
             raws[pair] = got
 
-        def copy_out(dst, src):
-            n = state["copies"]
-            state["copies"] = n + 1
-            if n % VEC_OF == VEC_OF - 1:
-                nc.vector.tensor_copy(out=dst, in_=src)
-            else:
-                nc.scalar.copy(out=dst, in_=src)
-
-        def prep(g):
+        def prep_first(g):
             h, b = divmod(g, NBLK)
             if b == 0:
                 kqs[h] = heads.tile([P, NBLK, 2 * BLK], BF16, name="kq", tag="kq")
@@ -83,120 +97,175 @@ def tile_blocksparseattention_t_kernel(tc, q, k, v, out):
                     nc.tensor.transpose(
                         out=tp[:, x * BLK + t * P:x * BLK + (t + 1) * P],
                         in_=src[:, b % 2, t * D:(t + 1) * D],
-                        identity=ident[:],
+                        identity=(ident[:] if x == 0 else perm[:]),
                     )
-            nc.scalar.copy(out=kqs[h][:, b, :], in_=tp[:])
             vg = work.tile([P, BLK], BF16, name="vg", tag="vg", align_bytes=64)
-            nc.gpsimd.tensor_scalar(
+            nc.vector.tensor_copy(
                 out=vg[:].rearrange("p (d t) -> p d t", t=PACK),
-                in0=vraw[:, b % 2, :].rearrange("p (t d) -> p d t", t=PACK),
-                scalar1=1.0, scalar2=0.0, op0=ALU.mult, op1=ALU.add,
+                in_=vraw[:, b % 2, :].rearrange("p (t d) -> p d t", t=PACK),
             )
+            preps[g] = (tp, vg)
+
+        def prep_second(g):
+            h, b = divmod(g, NBLK)
+            tp, vg = preps[g]
+            nc.scalar.copy(out=kqs[h][:, b, :], in_=tp[:])
             nc.vector.quantize_mx(
                 out=vcs[h][:, b * D:(b + 1) * D].bitcast(FP8X4),
                 scales=vss[h][:, b * D:(b + 1) * D],
                 in_=vg[:],
             )
 
-        def main(g):
+        def scores(n, c):
+            g, qt = divmod(n, PACK)
             h, i = divmod(g, NBLK)
-            lo = max(i - 1, 0)
-            ncb = min(i + 2, NBLK) - lo
-            kq = kqs[h]
-            units = PACK * ncb
-            codes = work.tile([P, PACK * 3 * P], U32, name="codes", tag="codes", align_bytes=64)
-            scl = work.tile([P, PACK * 3 * P], U8, name="scl", tag="scl", align_bytes=64)
-            rs = small.tile([P, PACK * 3], F32, name="rs", tag="rs")
-            tp = None
-            for qt in range(PACK):
-                mx = small.tile([P, 4], F32, name="mx", tag="mx")
-                ssb = work.tile([P, 3 * BLK], F32, name="ssb", tag="ssb")
-                for c in range(ncb):
-                    sp = ps_s.tile([P, BLK], F32, name="sp", tag="sp")
-                    nc.tensor.matmul(
-                        out=sp[:],
-                        lhsT=kq[:, i, BLK + qt * P:BLK + (qt + 1) * P],
-                        rhs=kq[:, lo + c, 0:BLK],
-                        start=True,
-                        stop=True,
+            lo, ncb = span(g)
+            if c == 0:
+                tiles[n] = {
+                    "mx": small.tile([P, 4], F32, name="mx", tag="mx"),
+                    "ssb": work.tile([P, 3 * BLK], F32, name="ssb", tag="ssb"),
+                }
+            sp = ps_s.tile([P, BLK], F32, name="sp", tag="sp")
+            nc.tensor.matmul(
+                out=sp[:],
+                lhsT=kqs[h][:, i, BLK + qt * P:BLK + (qt + 1) * P],
+                rhs=kqs[h][:, lo + c, 0:BLK],
+                start=True,
+                stop=True,
+            )
+            nc.vector.tensor_scalar(
+                out=tiles[n]["ssb"][:, c * BLK:(c + 1) * BLK], in0=sp[:], scalar1=-SCALE, scalar2=None,
+                op0=ALU.mult, op1=ALU.min, accum_out=tiles[n]["mx"][:, c:c + 1],
+            )
+
+        def shift(n):
+            ncb = span(n // PACK)[1]
+            mx = tiles[n]["mx"]
+            negm = small.tile([P, 1], F32, name="negm", tag="negm")
+            if ncb == 2:
+                nc.vector.tensor_scalar(
+                    out=negm[:], in0=mx[:, 0:1], scalar1=mx[:, 1:2], scalar2=None, op0=ALU.min,
+                )
+            else:
+                nc.vector.tensor_scalar(
+                    out=negm[:], in0=mx[:, 0:1], scalar1=mx[:, 1:2], scalar2=mx[:, 2:3],
+                    op0=ALU.min, op1=ALU.min,
+                )
+            tiles[n]["negm"] = negm
+
+        def exps(n):
+            g, qt = divmod(n, PACK)
+            ncb = span(g)[1]
+            if qt == 0:
+                blocks[g] = {
+                    "rs": small.tile([P, PACK * 3], F32, name="rs", tag="rs"),
+                    "e": work.tile([P, PACK, PACK, 3 * P], BF16, name="e", tag="e"),
+                }
+            e = blocks[g]["e"]
+            for c in range(ncb):
+                u = qt * ncb + c
+                nc.scalar.activation(
+                    out=e[:, qt, :, c * P:(c + 1) * P],
+                    in_=tiles[n]["ssb"][:, c * BLK:(c + 1) * BLK].rearrange("p (t k) -> p t k", t=PACK),
+                    func=ACT.Exp, bias=tiles[n]["negm"][:, 0:1], scale=-1.0,
+                    accum_out=blocks[g]["rs"][:, u:u + 1],
+                )
+
+        def shuffle(g):
+            ncb = span(g)[1]
+            e2 = work.tile([P, PACK, GRP, 3 * P], BF16, name="e2", tag="e2")
+            blocks[g]["e2"] = e2
+            for grp_i in range(GRP):
+                for t in range(PACK):
+                    nc.sync.dma_start(
+                        out=e2[t:P:PACK, :, grp_i, 0:ncb * P],
+                        in_=blocks[g]["e"][grp_i:P:GRP, :, t, 0:ncb * P],
                     )
-                    nc.vector.tensor_scalar(
-                        out=ssb[:, c * BLK:(c + 1) * BLK], in0=sp[:], scalar1=-SCALE, scalar2=None,
-                        op0=ALU.mult, op1=ALU.min, accum_out=mx[:, c:c + 1],
-                    )
-                negm = small.tile([P, 1], F32, name="negm", tag="negm")
-                if ncb == 2:
-                    nc.vector.tensor_scalar(
-                        out=negm[:], in0=mx[:, 0:1], scalar1=mx[:, 1:2], scalar2=None, op0=ALU.min,
-                    )
-                else:
-                    nc.vector.tensor_scalar(
-                        out=negm[:], in0=mx[:, 0:1], scalar1=mx[:, 1:2], scalar2=mx[:, 2:3],
-                        op0=ALU.min, op1=ALU.min,
-                    )
-                e = work.tile([P, 3 * BLK], BF16, name="e", tag="e")
-                for c in range(ncb):
-                    u = qt * ncb + c
-                    nc.scalar.activation(
-                        out=e[:, c * BLK:(c + 1) * BLK], in_=ssb[:, c * BLK:(c + 1) * BLK], func=ACT.Exp,
-                        bias=negm[:, 0:1], scale=-1.0, accum_out=rs[:, u:u + 1],
-                    )
-                for c in range(ncb):
-                    u = qt * ncb + c
-                    if u % 2 == 0:
-                        tp = ps_t.tile([P, 2 * BLK], BF16, name="tp", tag="tp")
-                    for t in range(PACK):
-                        nc.tensor.transpose(
-                            out=tp[:, (u % 2) * BLK + t * P:(u % 2) * BLK + (t + 1) * P],
-                            in_=e[:, c * BLK + t * P:c * BLK + (t + 1) * P],
-                            identity=ident[:],
-                        )
-                    if u % 2 == 1:
-                        grp = work.tile([P, 2 * BLK], BF16, name="grp", tag="grp", align_bytes=64)
-                        if X_MODE == "P1":
-                            copy_out(
-                                grp[:].rearrange("p (u q t) -> p u q t", u=2, t=PACK),
-                                tp[:].rearrange("p (u t q) -> p u q t", u=2, t=PACK),
-                            )
-                        else:
-                            pln = work.tile([P, 2 * BLK], BF16, name="pln", tag="pln")
-                            nc.scalar.copy(out=pln[:], in_=tp[:])
-                            nc.gpsimd.tensor_scalar(
-                                out=grp[:].rearrange("p (u q t) -> p u q t", u=2, t=PACK),
-                                in0=pln[:].rearrange("p (u t q) -> p u q t", u=2, t=PACK),
-                                scalar1=1.0, scalar2=0.0, op0=ALU.mult, op1=ALU.add,
-                            )
-                        w0 = (u - 1) * P
-                        nc.vector.quantize_mx(
-                            out=codes[:, w0:w0 + 2 * P].bitcast(FP8X4),
-                            scales=scl[:, w0:w0 + 2 * P],
-                            in_=grp[:],
-                        )
+
+        def turn(n, c, done):
+            g, qt = divmod(n, PACK)
+            ncb = span(g)[1]
+            u = qt * ncb + c
+            if u % 2 == 0:
+                state["tp"] = ps_t.tile([P, 2 * BLK], BF16, name="tp", tag="tp")
+            tp = state["tp"]
+            e2 = blocks[g]["e2"]
+            for grp_i in range(GRP):
+                nc.tensor.transpose(
+                    out=tp[:, (u % 2) * BLK + grp_i * P:(u % 2) * BLK + (grp_i + 1) * P],
+                    in_=e2[:, qt, grp_i, c * P:(c + 1) * P],
+                    identity=ident[:],
+                )
+            if u % 2 == 1:
+                done.append((g, u - 1, tp))
+
+        def choose(banks):
+            picked = []
+            for bank in banks:
+                cnt = state["copies"]
+                state["copies"] = cnt + 1
+                picked.append((bank, VEC_OF > 0 and cnt % VEC_OF == VEC_OF - 1))
+            return picked
+
+        def copy_out(bank, on_vector):
+            g, u0, tp = bank
+            grp = work.tile([P, 2 * BLK], BF16, name="grp", tag="grp", bufs=6, align_bytes=64)
+            if on_vector:
+                nc.vector.tensor_copy(out=grp[:], in_=tp[:])
+            else:
+                nc.scalar.copy(out=grp[:], in_=tp[:])
+            return (g, u0, grp)
+
+        def quantise(item):
+            g, u0, grp = item
+            if u0 == 0:
+                blocks[g]["codes"] = work.tile([P, PACK * 3 * P], U32, name="codes", tag="codes", align_bytes=64)
+                blocks[g]["scl"] = work.tile([P, PACK * 3 * P], U8, name="scl", tag="scl", align_bytes=64)
+            nc.vector.quantize_mx(
+                out=blocks[g]["codes"][:, u0 * P:(u0 + 2) * P].bitcast(FP8X4),
+                scales=blocks[g]["scl"][:, u0 * P:(u0 + 2) * P],
+                in_=grp[:],
+            )
+
+        def weighted(g):
+            h = g // NBLK
+            lo, ncb = span(g)
             pv = ps_o.tile([P, PACK * D], F32, name="pv", tag="pv")
+            blocks[g]["pv"] = pv
             for qt in range(PACK):
                 for c in range(ncb):
                     u = qt * ncb + c
                     nc.tensor.matmul_mx(
                         out=pv[:, qt * D:(qt + 1) * D],
-                        lhsT=codes[:, u * P:(u + 1) * P].bitcast(FP8X4),
-                        lhsT_scale=scl[:, u * P:(u + 1) * P],
+                        lhsT=blocks[g]["codes"][:, u * P:(u + 1) * P].bitcast(FP8X4),
+                        lhsT_scale=blocks[g]["scl"][:, u * P:(u + 1) * P],
                         rhs=vcs[h][:, (lo + c) * D:(lo + c + 1) * D].bitcast(FP8X4),
                         rhs_scale=vss[h][:, (lo + c) * D:(lo + c + 1) * D],
                         start=(c == 0),
                         stop=(c == ncb - 1),
                     )
+
+        def sums(g):
+            ncb = span(g)[1]
             rsum = small.tile([P, PACK], F32, name="rsum", tag="rsum")
             nc.vector.tensor_reduce(
-                out=rsum[:], in_=rs[:, 0:units].rearrange("p (a c) -> p a c", c=ncb),
+                out=rsum[:], in_=blocks[g]["rs"][:, 0:PACK * ncb].rearrange("p (a c) -> p a c", c=ncb),
                 axis=AX.X, op=ALU.add,
             )
             rinv = small.tile([P, PACK], F32, name="rinv", tag="rinv")
             nc.vector.reciprocal(out=rinv[:], in_=rsum[:])
+            rinv2 = small.tile([P, PACK], F32, name="rinv2", tag="rinv2")
+            for grp_i in range(GRP):
+                nc.sync.dma_start(out=rinv2[grp_i * QG:(grp_i + 1) * QG, :], in_=rinv[grp_i:P:GRP, :])
+            blocks[g]["rinv"] = rinv2
+
+        def finish(g):
+            h, i = divmod(g, NBLK)
             o_sb = work.tile([P, PACK * D], F32, name="o_sb", tag="o_sb")
             nc.vector.tensor_tensor(
                 out=o_sb[:].rearrange("p (a d) -> p a d", a=PACK),
-                in0=pv[:].rearrange("p (a d) -> p a d", a=PACK),
-                in1=rinv[:].unsqueeze(2).to_broadcast([P, PACK, D]),
+                in0=blocks[g]["pv"][:].rearrange("p (a d) -> p a d", a=PACK),
+                in1=blocks[g]["rinv"][:].unsqueeze(2).to_broadcast([P, PACK, D]),
                 op=ALU.mult,
             )
             nc.sync.dma_start(
@@ -204,15 +273,49 @@ def tile_blocksparseattention_t_kernel(tc, q, k, v, out):
                 in_=o_sb[:],
             )
 
-        total = H * NBLK
         load(0)
         load(1)
-        prep(0)
-        prep(1)
-        for g in range(total):
-            nxt = g + 2
-            if nxt < total:
-                if nxt % 2 == 0 and nxt // 2 + 1 < total // 2:
-                    load(nxt // 2 + 1)
-                prep(nxt)
-            main(g)
+        prep_first(0)
+        prep_second(0)
+        prep_first(1)
+        prep_second(1)
+
+        turned = {}
+        copied = {}
+        for it in range(ntiles + LAG + 8):
+            g4, r4 = divmod(it, PACK)
+            if r4 == 0 and g4 % 2 == 0 and g4 // 2 + 2 < total // 2:
+                load(g4 // 2 + 2)
+            done = []
+            for c in range(3):
+                if 0 <= it - LAG < ntiles and c < span((it - LAG) // PACK)[1]:
+                    turn(it - LAG, c, done)
+                if it < ntiles and c < span(it // PACK)[1]:
+                    scores(it, c)
+            turned[it] = choose(done)
+            if 0 <= it - 1 < ntiles:
+                exps(it - 1)
+                if r4 == 0:
+                    shuffle(g4 - 1)
+            got = []
+            for bank, on_vector in turned.get(it - 1, []):
+                if not on_vector:
+                    got.append(copy_out(bank, False))
+            if r4 == 1 and g4 + 2 < total:
+                prep_second(g4 + 2)
+            for item in copied.get(it - 1, []):
+                quantise(item)
+            for bank, on_vector in turned.get(it - 1, []):
+                if on_vector:
+                    got.append(copy_out(bank, True))
+            copied[it] = got
+            if it < ntiles:
+                shift(it)
+            if r4 == 3 and 0 <= g4 - 3 < total:
+                finish(g4 - 3)
+            if r4 == 1 and 0 <= g4 - 1 < total:
+                sums(g4 - 1)
+            if r4 == 2 and 0 <= g4 - 3 < total:
+                weighted(g4 - 3)
+            if r4 == 0 and g4 + 2 < total:
+                prep_first(g4 + 2)

@@ -28,7 +28,7 @@ VEC_OF = 0
 PINNED = True
 GRP = 4
 QG = P // GRP
-LAG = 8
+LAG = 12
 
 
 def tile_blocksparseattention_t_kernel(tc, q, k, v, out):
@@ -159,13 +159,13 @@ def tile_blocksparseattention_t_kernel(tc, q, k, v, out):
             if qt == 0:
                 blocks[g] = {
                     "rs": small.tile([P, PACK * 3], F32, name="rs", tag="rs"),
-                    "e": work.tile([P, PACK, PACK, 3 * P], BF16, name="e", tag="e"),
+                    "e": work.tile([P, PACK, PACK, ncb * P], BF16, name="e", tag="e", bufs=2),
                 }
             e = blocks[g]["e"]
             for c in range(ncb):
                 u = qt * ncb + c
                 nc.scalar.activation(
-                    out=e[:, qt, :, c * P:(c + 1) * P],
+                    out=e[:, :, qt, c * P:(c + 1) * P],
                     in_=tiles[n]["ssb"][:, c * BLK:(c + 1) * BLK].rearrange("p (t k) -> p t k", t=PACK),
                     func=ACT.Exp, bias=tiles[n]["negm"][:, 0:1], scale=-1.0,
                     accum_out=blocks[g]["rs"][:, u:u + 1],
@@ -173,13 +173,13 @@ def tile_blocksparseattention_t_kernel(tc, q, k, v, out):
 
         def shuffle(g):
             ncb = span(g)[1]
-            e2 = work.tile([P, PACK, GRP, 3 * P], BF16, name="e2", tag="e2")
+            e2 = work.tile([P, GRP, PACK, ncb * P], BF16, name="e2", tag="e2", bufs=4)
             blocks[g]["e2"] = e2
             for grp_i in range(GRP):
                 for t in range(PACK):
                     nc.sync.dma_start(
-                        out=e2[t:P:PACK, :, grp_i, 0:ncb * P],
-                        in_=blocks[g]["e"][grp_i:P:GRP, :, t, 0:ncb * P],
+                        out=e2[t:P:PACK, grp_i, :, :],
+                        in_=blocks[g]["e"][grp_i:P:GRP, t, :, :],
                     )
 
         def turn(n, c, done):
@@ -193,7 +193,7 @@ def tile_blocksparseattention_t_kernel(tc, q, k, v, out):
             for grp_i in range(GRP):
                 nc.tensor.transpose(
                     out=tp[:, (u % 2) * BLK + grp_i * P:(u % 2) * BLK + (grp_i + 1) * P],
-                    in_=e2[:, qt, grp_i, c * P:(c + 1) * P],
+                    in_=e2[:, grp_i, qt, c * P:(c + 1) * P],
                     identity=ident[:],
                 )
             if u % 2 == 1:
@@ -254,7 +254,7 @@ def tile_blocksparseattention_t_kernel(tc, q, k, v, out):
             )
             rinv = small.tile([P, PACK], F32, name="rinv", tag="rinv")
             nc.vector.reciprocal(out=rinv[:], in_=rsum[:])
-            rinv2 = small.tile([P, PACK], F32, name="rinv2", tag="rinv2")
+            rinv2 = small.tile([P, PACK], F32, name="rinv2", tag="rinv2", bufs=6)
             for grp_i in range(GRP):
                 nc.sync.dma_start(out=rinv2[grp_i * QG:(grp_i + 1) * QG, :], in_=rinv[grp_i:P:GRP, :])
             blocks[g]["rinv"] = rinv2
@@ -288,34 +288,34 @@ def tile_blocksparseattention_t_kernel(tc, q, k, v, out):
                 load(g4 // 2 + 2)
             done = []
             for c in range(3):
-                if 0 <= it - LAG < ntiles and c < span((it - LAG) // PACK)[1]:
-                    turn(it - LAG, c, done)
                 if it < ntiles and c < span(it // PACK)[1]:
                     scores(it, c)
+                if 0 <= it - LAG < ntiles and c < span((it - LAG) // PACK)[1]:
+                    turn(it - LAG, c, done)
             turned[it] = choose(done)
             if 0 <= it - 1 < ntiles:
                 exps(it - 1)
                 if r4 == 0:
                     shuffle(g4 - 1)
             got = []
-            for bank, on_vector in turned.get(it - 1, []):
+            for bank, on_vector in turned.get(it, []):
                 if not on_vector:
                     got.append(copy_out(bank, False))
             if r4 == 1 and g4 + 2 < total:
                 prep_second(g4 + 2)
             for item in copied.get(it - 1, []):
                 quantise(item)
-            for bank, on_vector in turned.get(it - 1, []):
+            for bank, on_vector in turned.get(it, []):
                 if on_vector:
                     got.append(copy_out(bank, True))
             copied[it] = got
             if it < ntiles:
                 shift(it)
-            if r4 == 3 and 0 <= g4 - 3 < total:
-                finish(g4 - 3)
+            if r4 == 3 and 0 <= g4 - 4 < total:
+                finish(g4 - 4)
             if r4 == 1 and 0 <= g4 - 1 < total:
                 sums(g4 - 1)
-            if r4 == 2 and 0 <= g4 - 3 < total:
-                weighted(g4 - 3)
+            if r4 == 2 and 0 <= g4 - 4 < total:
+                weighted(g4 - 4)
             if r4 == 0 and g4 + 2 < total:
                 prep_first(g4 + 2)

@@ -143,11 +143,11 @@ def tile_blocksparseattention_t_kernel(tc, q, k, v, out):
             mx = tiles[n]["mx"]
             negm = small.tile([P, 1], F32, name="negm", tag="negm")
             if ncb == 2:
-                nc.vector.tensor_scalar(
+                nc.gpsimd.tensor_scalar(
                     out=negm[:], in0=mx[:, 0:1], scalar1=mx[:, 1:2], scalar2=None, op0=ALU.min,
                 )
             else:
-                nc.vector.tensor_scalar(
+                nc.gpsimd.tensor_scalar(
                     out=negm[:], in0=mx[:, 0:1], scalar1=mx[:, 1:2], scalar2=mx[:, 2:3],
                     op0=ALU.min, op1=ALU.min,
                 )
@@ -158,18 +158,16 @@ def tile_blocksparseattention_t_kernel(tc, q, k, v, out):
             ncb = span(g)[1]
             if qt == 0:
                 blocks[g] = {
-                    "rs": small.tile([P, PACK * 3], F32, name="rs", tag="rs"),
+                    "rs": small.tile([P, PACK], F32, name="rs", tag="rs"),
                     "e": work.tile([P, PACK, PACK, ncb * P], BF16, name="e", tag="e", bufs=2),
                 }
             e = blocks[g]["e"]
-            for c in range(ncb):
-                u = qt * ncb + c
-                nc.scalar.activation(
-                    out=e[:, :, qt, c * P:(c + 1) * P],
-                    in_=tiles[n]["ssb"][:, c * BLK:(c + 1) * BLK].rearrange("p (t k) -> p t k", t=PACK),
-                    func=ACT.Exp, bias=tiles[n]["negm"][:, 0:1], scale=-1.0,
-                    accum_out=blocks[g]["rs"][:, u:u + 1],
-                )
+            nc.scalar.activation(
+                out=e[:, :, qt, :].rearrange("p t (c k) -> p t c k", c=ncb),
+                in_=tiles[n]["ssb"][:, 0:ncb * BLK].rearrange("p (c t k) -> p t c k", c=ncb, t=PACK),
+                func=ACT.Exp, bias=tiles[n]["negm"][:, 0:1], scale=-1.0,
+                accum_out=blocks[g]["rs"][:, qt:qt + 1],
+            )
 
         def shuffle(g):
             ncb = span(g)[1]
@@ -246,14 +244,8 @@ def tile_blocksparseattention_t_kernel(tc, q, k, v, out):
                     )
 
         def sums(g):
-            ncb = span(g)[1]
-            rsum = small.tile([P, PACK], F32, name="rsum", tag="rsum")
-            nc.vector.tensor_reduce(
-                out=rsum[:], in_=blocks[g]["rs"][:, 0:PACK * ncb].rearrange("p (a c) -> p a c", c=ncb),
-                axis=AX.X, op=ALU.add,
-            )
             rinv = small.tile([P, PACK], F32, name="rinv", tag="rinv")
-            nc.vector.reciprocal(out=rinv[:], in_=rsum[:])
+            nc.vector.reciprocal(out=rinv[:], in_=blocks[g]["rs"][:])
             rinv2 = small.tile([P, PACK], F32, name="rinv2", tag="rinv2", bufs=6)
             for grp_i in range(GRP):
                 nc.sync.dma_start(out=rinv2[grp_i * QG:(grp_i + 1) * QG, :], in_=rinv[grp_i:P:GRP, :])

@@ -101,8 +101,8 @@ def tile_blocksparseattention_t_kernel(tc, q, k, v, out):
                     )
             vg = work.tile([P, BLK], BF16, name="vg", tag="vg", align_bytes=64)
             nc.vector.tensor_copy(
-                out=vg[:].rearrange("p (d t) -> p d t", t=PACK),
-                in_=vraw[:, b % 2, :].rearrange("p (t d) -> p d t", t=PACK),
+                out=vg[:].rearrange("p (c i t) -> p c t i", i=4, t=PACK),
+                in_=vraw[:, b % 2, :].rearrange("p (t c i) -> p c t i", t=PACK, i=4),
             )
             preps[g] = (tp, vg)
 
@@ -123,7 +123,7 @@ def tile_blocksparseattention_t_kernel(tc, q, k, v, out):
             if c == 0:
                 tiles[n] = {
                     "mx": small.tile([P, 4], F32, name="mx", tag="mx"),
-                    "ssb": work.tile([P, 3 * BLK], F32, name="ssb", tag="ssb"),
+                    "ssb": work.tile([P, 3 * BLK], F32, name="ssb", tag="ssb", bufs=4),
                 }
             sp = ps_s.tile([P, BLK], F32, name="sp", tag="sp")
             nc.tensor.matmul(
@@ -285,9 +285,9 @@ def tile_blocksparseattention_t_kernel(tc, q, k, v, out):
                 if 0 <= it - LAG < ntiles and c < span((it - LAG) // PACK)[1]:
                     turn(it - LAG, c, done)
             turned[it] = choose(done)
-            if 0 <= it - 1 < ntiles:
-                exps(it - 1)
-                if r4 == 0:
+            if 0 <= it - 2 < ntiles:
+                exps(it - 2)
+                if r4 == 1:
                     shuffle(g4 - 1)
             got = []
             for bank, on_vector in turned.get(it, []):
@@ -305,7 +305,7 @@ def tile_blocksparseattention_t_kernel(tc, q, k, v, out):
                 shift(it)
             if r4 == 3 and 0 <= g4 - 4 < total:
                 finish(g4 - 4)
-            if r4 == 1 and 0 <= g4 - 1 < total:
+            if r4 == 2 and 0 <= g4 - 1 < total:
                 sums(g4 - 1)
             if r4 == 2 and 0 <= g4 - 4 < total:
                 weighted(g4 - 4)

@@ -11,7 +11,6 @@ U8 = mybir.dt.uint8
 FP8X4 = mybir.dt.float8_e4m3fn_x4
 ALU = mybir.AluOpType
 ACT = mybir.ActivationFunctionType
-AX = mybir.AxisListType
 
 H = 4
 S = 4096
@@ -25,10 +24,9 @@ FLOPS = 2 * 2 * PAIRS * BLK * BLK * D
 SCALE = 1.0 / math.sqrt(D)
 
 VEC_OF = 0
-PINNED = True
-GRP = 4
-QG = P // GRP
-LAG = 12
+LT = 4
+V_ON_G = False
+HW = BLK // 2
 
 
 def tile_blocksparseattention_t_kernel(tc, q, k, v, out):
@@ -45,15 +43,10 @@ def tile_blocksparseattention_t_kernel(tc, q, k, v, out):
 
         ident = const.tile([P, P], BF16, name="ident")
         make_identity(nc, ident[:])
+        identf = const.tile([P, P], F32, name="identf")
+        make_identity(nc, identf[:])
 
-        perm = const.tile([P, P], BF16, name="perm")
-        nc.vector.tensor_copy(
-            out=perm[:].rearrange("p (q g) -> p q g", g=GRP),
-            in_=ident[:].rearrange("p (g q) -> p q g", g=GRP),
-        )
-
-        if PINNED:
-            ctx.enter_context(tc.manual_schedule())
+        ctx.enter_context(tc.manual_schedule())
 
         total = H * NBLK
         ntiles = total * PACK
@@ -73,9 +66,17 @@ def tile_blocksparseattention_t_kernel(tc, q, k, v, out):
 
         def load(pair):
             h, b2 = divmod(pair, NBLK // 2)
-            rows = slice(b2 * 2 * BLK, (b2 + 1) * 2 * BLK)
-            got = []
-            for nm, src in (("kraw", k), ("qraw", q), ("vraw", v)):
+            r0 = b2 * 2 * BLK
+            rows = slice(r0, r0 + 2 * BLK)
+            kraw = raw.tile([P, 4, 2, D], BF16, name="kraw", tag="kraw")
+            for u in range(2):
+                for e in range(2):
+                    nc.sync.dma_start(
+                        out=kraw[e:P:2, :, u, :],
+                        in_=k[0, h, r0 + 2 * u + e:r0 + 2 * BLK:4, :].rearrange("(a j) d -> j a d", j=P // 2),
+                    )
+            got = [kraw]
+            for nm, src in (("qraw", q), ("vraw", v)):
                 t = raw.tile([P, 2, BLK], BF16, name=nm, tag=nm)
                 nc.sync.dma_start(
                     out=t[:],
@@ -92,15 +93,22 @@ def tile_blocksparseattention_t_kernel(tc, q, k, v, out):
                 vss[h] = heads.tile([P, NBLK * D], U8, name="vscales", tag="vscales", align_bytes=64)
             kraw, qraw, vraw = raws[g // 2]
             tp = ps_t.tile([P, 2 * BLK], BF16, name="tp", tag="tp")
-            for x, src in enumerate((kraw, qraw)):
-                for t in range(PACK):
+            for u in range(2):
+                for a in range(2):
                     nc.tensor.transpose(
-                        out=tp[:, x * BLK + t * P:x * BLK + (t + 1) * P],
-                        in_=src[:, b % 2, t * D:(t + 1) * D],
-                        identity=(ident[:] if x == 0 else perm[:]),
+                        out=tp[:, u * HW + a * P:u * HW + (a + 1) * P],
+                        in_=kraw[:, (b % 2) * 2 + a, u, :],
+                        identity=ident[:],
                     )
+            for t in range(PACK):
+                nc.tensor.transpose(
+                    out=tp[:, BLK + t * P:BLK + (t + 1) * P],
+                    in_=qraw[:, b % 2, t * D:(t + 1) * D],
+                    identity=ident[:],
+                )
             vg = work.tile([P, BLK], BF16, name="vg", tag="vg", align_bytes=64)
-            nc.vector.tensor_copy(
+            eng = nc.gpsimd if V_ON_G else nc.vector
+            eng.tensor_copy(
                 out=vg[:].rearrange("p (c i t) -> p c t i", i=4, t=PACK),
                 in_=vraw[:, b % 2, :].rearrange("p (t c i) -> p c t i", t=PACK, i=4),
             )
@@ -109,7 +117,7 @@ def tile_blocksparseattention_t_kernel(tc, q, k, v, out):
         def prep_second(g):
             h, b = divmod(g, NBLK)
             tp, vg = preps[g]
-            nc.scalar.copy(out=kqs[h][:, b, :], in_=tp[:])
+            nc.scalar.copy(out=kqs[h][:, b, :].bitcast(F32), in_=tp[:].bitcast(F32))
             nc.vector.quantize_mx(
                 out=vcs[h][:, b * D:(b + 1) * D].bitcast(FP8X4),
                 scales=vss[h][:, b * D:(b + 1) * D],
@@ -157,42 +165,29 @@ def tile_blocksparseattention_t_kernel(tc, q, k, v, out):
             g, qt = divmod(n, PACK)
             ncb = span(g)[1]
             if qt == 0:
-                blocks[g] = {
-                    "rs": small.tile([P, PACK], F32, name="rs", tag="rs"),
-                    "e": work.tile([P, PACK, PACK, ncb * P], BF16, name="e", tag="e", bufs=2),
-                }
-            e = blocks[g]["e"]
+                blocks[g] = {"rs": small.tile([P, PACK], F32, name="rs", tag="rs")}
+            e = work.tile([P, 3 * BLK], BF16, name="e", tag="e", bufs=LT)
+            tiles[n]["e"] = e
             nc.scalar.activation(
-                out=e[:, :, qt, :].rearrange("p t (c k) -> p t c k", c=ncb),
-                in_=tiles[n]["ssb"][:, 0:ncb * BLK].rearrange("p (c t k) -> p t c k", c=ncb, t=PACK),
+                out=e[:, 0:ncb * BLK],
+                in_=tiles[n]["ssb"][:, 0:ncb * BLK],
                 func=ACT.Exp, bias=tiles[n]["negm"][:, 0:1], scale=-1.0,
                 accum_out=blocks[g]["rs"][:, qt:qt + 1],
             )
-
-        def shuffle(g):
-            ncb = span(g)[1]
-            e2 = work.tile([P, GRP, PACK, ncb * P], BF16, name="e2", tag="e2", bufs=4)
-            blocks[g]["e2"] = e2
-            for grp_i in range(GRP):
-                for t in range(PACK):
-                    nc.sync.dma_start(
-                        out=e2[t:P:PACK, grp_i, :, :],
-                        in_=blocks[g]["e"][grp_i:P:GRP, t, :, :],
-                    )
 
         def turn(n, c, done):
             g, qt = divmod(n, PACK)
             ncb = span(g)[1]
             u = qt * ncb + c
             if u % 2 == 0:
-                state["tp"] = ps_t.tile([P, 2 * BLK], BF16, name="tp", tag="tp")
+                state["tp"] = ps_t.tile([P, BLK], F32, name="tp", tag="tp")
             tp = state["tp"]
-            e2 = blocks[g]["e2"]
-            for grp_i in range(GRP):
+            words = tiles[n]["e"][:].bitcast(F32)
+            for w in range(2):
                 nc.tensor.transpose(
-                    out=tp[:, (u % 2) * BLK + grp_i * P:(u % 2) * BLK + (grp_i + 1) * P],
-                    in_=e2[:, grp_i, qt, c * P:(c + 1) * P],
-                    identity=ident[:],
+                    out=tp[:, (u % 2) * HW + w * P:(u % 2) * HW + (w + 1) * P],
+                    in_=words[:, c * HW + w * P:c * HW + (w + 1) * P],
+                    identity=identf[:],
                 )
             if u % 2 == 1:
                 done.append((g, u - 1, tp))
@@ -208,10 +203,12 @@ def tile_blocksparseattention_t_kernel(tc, q, k, v, out):
         def copy_out(bank, on_vector):
             g, u0, tp = bank
             grp = work.tile([P, 2 * BLK], BF16, name="grp", tag="grp", bufs=6, align_bytes=64)
+            dst = grp[:].bitcast(F32).rearrange("p (a q w) -> p a q w", a=2, w=2)
+            src = tp[:].rearrange("p (a w q) -> p a q w", a=2, w=2)
             if on_vector:
-                nc.vector.tensor_copy(out=grp[:], in_=tp[:])
+                nc.vector.tensor_copy(out=dst, in_=src)
             else:
-                nc.scalar.copy(out=grp[:], in_=tp[:])
+                nc.scalar.copy(out=dst, in_=src)
             return (g, u0, grp)
 
         def quantise(item):
@@ -246,10 +243,7 @@ def tile_blocksparseattention_t_kernel(tc, q, k, v, out):
         def sums(g):
             rinv = small.tile([P, PACK], F32, name="rinv", tag="rinv")
             nc.vector.reciprocal(out=rinv[:], in_=blocks[g]["rs"][:])
-            rinv2 = small.tile([P, PACK], F32, name="rinv2", tag="rinv2", bufs=6)
-            for grp_i in range(GRP):
-                nc.sync.dma_start(out=rinv2[grp_i * QG:(grp_i + 1) * QG, :], in_=rinv[grp_i:P:GRP, :])
-            blocks[g]["rinv"] = rinv2
+            blocks[g]["rinv"] = rinv
 
         def finish(g):
             h, i = divmod(g, NBLK)
@@ -272,9 +266,10 @@ def tile_blocksparseattention_t_kernel(tc, q, k, v, out):
         prep_first(1)
         prep_second(1)
 
+        GL = (LT + 3) // PACK + 1
         turned = {}
         copied = {}
-        for it in range(ntiles + LAG + 8):
+        for it in range(ntiles + PACK * GL + PACK):
             g4, r4 = divmod(it, PACK)
             if r4 == 0 and g4 % 2 == 0 and g4 // 2 + 2 < total // 2:
                 load(g4 // 2 + 2)
@@ -282,13 +277,11 @@ def tile_blocksparseattention_t_kernel(tc, q, k, v, out):
             for c in range(3):
                 if it < ntiles and c < span(it // PACK)[1]:
                     scores(it, c)
-                if 0 <= it - LAG < ntiles and c < span((it - LAG) // PACK)[1]:
-                    turn(it - LAG, c, done)
+                if 0 <= it - LT < ntiles and c < span((it - LT) // PACK)[1]:
+                    turn(it - LT, c, done)
             turned[it] = choose(done)
             if 0 <= it - 2 < ntiles:
                 exps(it - 2)
-                if r4 == 1:
-                    shuffle(g4 - 1)
             got = []
             for bank, on_vector in turned.get(it, []):
                 if not on_vector:
@@ -303,11 +296,11 @@ def tile_blocksparseattention_t_kernel(tc, q, k, v, out):
             copied[it] = got
             if it < ntiles:
                 shift(it)
-            if r4 == 3 and 0 <= g4 - 4 < total:
-                finish(g4 - 4)
+            if r4 == 3 and 0 <= g4 - GL < total:
+                finish(g4 - GL)
             if r4 == 2 and 0 <= g4 - 1 < total:
                 sums(g4 - 1)
-            if r4 == 2 and 0 <= g4 - 4 < total:
-                weighted(g4 - 4)
+            if r4 == 2 and 0 <= g4 - GL < total:
+                weighted(g4 - GL)
             if r4 == 0 and g4 + 2 < total:
                 prep_first(g4 + 2)

@@ -25,7 +25,7 @@ SCALE = 1.0 / math.sqrt(D)
 
 VEC_OF = 0
 LT = 4
-V_ON_G = False
+V_ON_G = True
 HW = BLK // 2
 
 

@@ -23,9 +23,10 @@ PAIRS = H * (3 * NBLK - 2)
 FLOPS = 2 * 2 * PAIRS * BLK * BLK * D
 SCALE = 1.0 / math.sqrt(D)
 
-VEC_OF = 0
+VEC_OF = 16
 LT = 4
 V_ON_G = True
+TAIL_V = 0
 HW = BLK // 2
 
 
@@ -192,12 +193,12 @@ def tile_blocksparseattention_t_kernel(tc, q, k, v, out):
             if u % 2 == 1:
                 done.append((g, u - 1, tp))
 
-        def choose(banks):
+        def choose(banks, tail):
             picked = []
             for bank in banks:
                 cnt = state["copies"]
                 state["copies"] = cnt + 1
-                picked.append((bank, VEC_OF > 0 and cnt % VEC_OF == VEC_OF - 1))
+                picked.append((bank, tail or (VEC_OF > 0 and cnt % VEC_OF == VEC_OF - 1)))
             return picked
 
         def copy_out(bank, on_vector):
@@ -279,7 +280,7 @@ def tile_blocksparseattention_t_kernel(tc, q, k, v, out):
                     scores(it, c)
                 if 0 <= it - LT < ntiles and c < span((it - LT) // PACK)[1]:
                     turn(it - LT, c, done)
-            turned[it] = choose(done)
+            turned[it] = choose(done, it >= ntiles + TAIL_V)
             if 0 <= it - 2 < ntiles:
                 exps(it - 2)
             got = []

@@ -25,8 +25,7 @@ SCALE = 1.0 / math.sqrt(D)
 
 VEC_OF = 16
 LT = 4
-V_ON_G = True
-TAIL_V = 0
+CATCH_UP = 3
 HW = BLK // 2
 
 
@@ -51,11 +50,13 @@ def tile_blocksparseattention_t_kernel(tc, q, k, v, out):
 
         total = H * NBLK
         ntiles = total * PACK
+        last = ntiles - 1
         raws = {}
         kqs = {}
         vcs = {}
         vss = {}
         preps = {}
+        vgs = {}
         blocks = {}
         tiles = {}
         state = {"copies": 0, "tp": None}
@@ -65,64 +66,88 @@ def tile_blocksparseattention_t_kernel(tc, q, k, v, out):
             lo = max(i - 1, 0)
             return lo, min(i + 2, NBLK) - lo
 
-        def load(pair):
+        def load_k(pair, b0, nb):
             h, b2 = divmod(pair, NBLK // 2)
-            r0 = b2 * 2 * BLK
-            rows = slice(r0, r0 + 2 * BLK)
-            kraw = raw.tile([P, 4, 2, D], BF16, name="kraw", tag="kraw")
+            r0 = (b2 * 2 + b0) * BLK
+            kraw = raws[pair][0]
             for u in range(2):
                 for e in range(2):
                     nc.sync.dma_start(
-                        out=kraw[e:P:2, :, u, :],
-                        in_=k[0, h, r0 + 2 * u + e:r0 + 2 * BLK:4, :].rearrange("(a j) d -> j a d", j=P // 2),
+                        out=kraw[e:P:2, 2 * b0:2 * (b0 + nb), u, :],
+                        in_=k[0, h, r0 + 2 * u + e:r0 + nb * BLK:4, :].rearrange("(a j) d -> j a d", j=P // 2),
                     )
-            got = [kraw]
-            for nm, src in (("qraw", q), ("vraw", v)):
-                t = raw.tile([P, 2, BLK], BF16, name=nm, tag=nm)
-                nc.sync.dma_start(
-                    out=t[:],
-                    in_=src[0, h, rows, :].rearrange("(b p t) d -> p b (t d)", b=2, p=P, t=PACK),
-                )
-                got.append(t)
-            raws[pair] = got
 
-        def prep_first(g):
+        def load_rows(pair, which, src, b0, nb, eng):
+            h, b2 = divmod(pair, NBLK // 2)
+            r0 = (b2 * 2 + b0) * BLK
+            eng.dma_start(
+                out=raws[pair][which][:, b0:b0 + nb, :],
+                in_=src[0, h, r0:r0 + nb * BLK, :].rearrange("(b p t) d -> p b (t d)", b=nb, p=P, t=PACK),
+            )
+
+        def new_raws(pair):
+            kraw = raw.tile([P, 4, 2, D], BF16, name="kraw", tag="kraw")
+            qraw = raw.tile([P, 2, BLK], BF16, name="qraw", tag="qraw")
+            vraw = raw.tile([P, 2, BLK], BF16, name="vraw", tag="vraw")
+            raws[pair] = (kraw, qraw, vraw)
+
+        def load(pair):
+            new_raws(pair)
+            load_k(pair, 0, 2)
+            load_rows(pair, 1, q, 0, 2, nc.sync)
+            load_rows(pair, 2, v, 0, 2, nc.sync)
+
+        def new_head(g):
             h, b = divmod(g, NBLK)
             if b == 0:
                 kqs[h] = heads.tile([P, NBLK, 2 * BLK], BF16, name="kq", tag="kq")
                 vcs[h] = heads.tile([P, NBLK * D], U32, name="vcodes", tag="vcodes", align_bytes=64)
                 vss[h] = heads.tile([P, NBLK * D], U8, name="vscales", tag="vscales", align_bytes=64)
-            kraw, qraw, vraw = raws[g // 2]
-            tp = ps_t.tile([P, 2 * BLK], BF16, name="tp", tag="tp")
+
+        def turn_k(g, tp):
+            kraw = raws[g // 2][0]
             for u in range(2):
                 for a in range(2):
                     nc.tensor.transpose(
                         out=tp[:, u * HW + a * P:u * HW + (a + 1) * P],
-                        in_=kraw[:, (b % 2) * 2 + a, u, :],
+                        in_=kraw[:, (g % 2) * 2 + a, u, :],
                         identity=ident[:],
                     )
+
+        def turn_q(g, tp, at):
+            qraw = raws[g // 2][1]
             for t in range(PACK):
                 nc.tensor.transpose(
-                    out=tp[:, BLK + t * P:BLK + (t + 1) * P],
-                    in_=qraw[:, b % 2, t * D:(t + 1) * D],
+                    out=tp[:, at + t * P:at + (t + 1) * P],
+                    in_=qraw[:, g % 2, t * D:(t + 1) * D],
                     identity=ident[:],
                 )
-            vg = work.tile([P, BLK], BF16, name="vg", tag="vg", align_bytes=64)
-            eng = nc.gpsimd if V_ON_G else nc.vector
-            eng.tensor_copy(
-                out=vg[:].rearrange("p (c i t) -> p c t i", i=4, t=PACK),
-                in_=vraw[:, b % 2, :].rearrange("p (t c i) -> p c t i", t=PACK, i=4),
-            )
-            preps[g] = (tp, vg)
+
+        def prep_first(g):
+            new_head(g)
+            tp = ps_t.tile([P, 2 * BLK], BF16, name="tp", tag="tp")
+            turn_k(g, tp)
+            turn_q(g, tp, BLK)
+            preps[g] = tp
 
         def prep_second(g):
             h, b = divmod(g, NBLK)
-            tp, vg = preps[g]
-            nc.scalar.copy(out=kqs[h][:, b, :].bitcast(F32), in_=tp[:].bitcast(F32))
+            nc.scalar.copy(out=kqs[h][:, b, :].bitcast(F32), in_=preps[g][:].bitcast(F32))
+
+        def v_first(g):
+            vg = work.tile([P, BLK], BF16, name="vg", tag="vg", align_bytes=64)
+            nc.gpsimd.tensor_copy(
+                out=vg[:].rearrange("p (c i t) -> p c t i", i=4, t=PACK),
+                in_=raws[g // 2][2][:, g % 2, :].rearrange("p (t c i) -> p c t i", t=PACK, i=4),
+            )
+            vgs[g] = vg
+
+        def v_second(g):
+            h, b = divmod(g, NBLK)
             nc.vector.quantize_mx(
                 out=vcs[h][:, b * D:(b + 1) * D].bitcast(FP8X4),
                 scales=vss[h][:, b * D:(b + 1) * D],
-                in_=vg[:],
+                in_=vgs[g][:],
             )
 
         def scores(n, c):
@@ -162,77 +187,78 @@ def tile_blocksparseattention_t_kernel(tc, q, k, v, out):
                 )
             tiles[n]["negm"] = negm
 
+        def exp(n, c0, c1, total_out):
+            nc.scalar.activation(
+                out=tiles[n]["e"][:, c0 * BLK:c1 * BLK],
+                in_=tiles[n]["ssb"][:, c0 * BLK:c1 * BLK],
+                func=ACT.Exp, bias=tiles[n]["negm"][:, 0:1], scale=-1.0,
+                accum_out=total_out,
+            )
+
         def exps(n):
             g, qt = divmod(n, PACK)
             ncb = span(g)[1]
             if qt == 0:
                 blocks[g] = {"rs": small.tile([P, PACK], F32, name="rs", tag="rs")}
-            e = work.tile([P, 3 * BLK], BF16, name="e", tag="e", bufs=LT)
-            tiles[n]["e"] = e
-            nc.scalar.activation(
-                out=e[:, 0:ncb * BLK],
-                in_=tiles[n]["ssb"][:, 0:ncb * BLK],
-                func=ACT.Exp, bias=tiles[n]["negm"][:, 0:1], scale=-1.0,
-                accum_out=blocks[g]["rs"][:, qt:qt + 1],
-            )
+            tiles[n]["e"] = work.tile([P, 3 * BLK], BF16, name="e", tag="e", bufs=LT)
+            if n < last:
+                exp(n, 0, ncb, blocks[g]["rs"][:, qt:qt + 1])
+            else:
+                parts = small.tile([P, 2], F32, name="parts", tag="parts")
+                exp(n, 0, 1, parts[:, 0:1])
+                exp(n, 1, 2, parts[:, 1:2])
+                nc.gpsimd.tensor_tensor(
+                    out=blocks[g]["rs"][:, qt:qt + 1], in0=parts[:, 0:1], in1=parts[:, 1:2], op=ALU.add,
+                )
 
-        def turn(n, c, done):
-            g, qt = divmod(n, PACK)
-            ncb = span(g)[1]
-            u = qt * ncb + c
-            if u % 2 == 0:
-                state["tp"] = ps_t.tile([P, BLK], F32, name="tp", tag="tp")
-            tp = state["tp"]
+        def turn_chunk(n, c, tp, at):
             words = tiles[n]["e"][:].bitcast(F32)
             for w in range(2):
                 nc.tensor.transpose(
-                    out=tp[:, (u % 2) * HW + w * P:(u % 2) * HW + (w + 1) * P],
+                    out=tp[:, at + w * P:at + (w + 1) * P],
                     in_=words[:, c * HW + w * P:c * HW + (w + 1) * P],
                     identity=identf[:],
                 )
-            if u % 2 == 1:
-                done.append((g, u - 1, tp))
 
-        def choose(banks, tail):
-            picked = []
-            for bank in banks:
-                cnt = state["copies"]
-                state["copies"] = cnt + 1
-                picked.append((bank, tail or (VEC_OF > 0 and cnt % VEC_OF == VEC_OF - 1)))
-            return picked
+        def turn(n, c, done):
+            g, qt = divmod(n, PACK)
+            u = qt * span(g)[1] + c
+            if u % 2 == 0:
+                state["tp"] = ps_t.tile([P, BLK], F32, name="tp", tag="tp")
+            turn_chunk(n, c, state["tp"], (u % 2) * HW)
+            if u % 2 == 1:
+                done.append((g, u - 1, state["tp"]))
+
+        def copy_words(eng_copy, grp, tp, a):
+            eng_copy(
+                out=grp.bitcast(F32).rearrange("p (a q w) -> p a q w", a=a, w=2),
+                in_=tp.rearrange("p (a w q) -> p a q w", a=a, w=2),
+            )
 
         def copy_out(bank, on_vector):
             g, u0, tp = bank
             grp = work.tile([P, 2 * BLK], BF16, name="grp", tag="grp", bufs=6, align_bytes=64)
-            dst = grp[:].bitcast(F32).rearrange("p (a q w) -> p a q w", a=2, w=2)
-            src = tp[:].rearrange("p (a w q) -> p a q w", a=2, w=2)
-            if on_vector:
-                nc.vector.tensor_copy(out=dst, in_=src)
-            else:
-                nc.scalar.copy(out=dst, in_=src)
+            copy_words(nc.vector.tensor_copy if on_vector else nc.scalar.copy, grp[:], tp[:], 2)
             return (g, u0, grp)
 
-        def quantise(item):
-            g, u0, grp = item
+        def quantise_units(g, u0, u1, src):
             if u0 == 0:
                 blocks[g]["codes"] = work.tile([P, PACK * 3 * P], U32, name="codes", tag="codes", align_bytes=64)
                 blocks[g]["scl"] = work.tile([P, PACK * 3 * P], U8, name="scl", tag="scl", align_bytes=64)
             nc.vector.quantize_mx(
-                out=blocks[g]["codes"][:, u0 * P:(u0 + 2) * P].bitcast(FP8X4),
-                scales=blocks[g]["scl"][:, u0 * P:(u0 + 2) * P],
-                in_=grp[:],
+                out=blocks[g]["codes"][:, u0 * P:u1 * P].bitcast(FP8X4),
+                scales=blocks[g]["scl"][:, u0 * P:u1 * P],
+                in_=src,
             )
 
-        def weighted(g):
+        def weighted(g, qts, pv):
             h = g // NBLK
             lo, ncb = span(g)
-            pv = ps_o.tile([P, PACK * D], F32, name="pv", tag="pv")
-            blocks[g]["pv"] = pv
-            for qt in range(PACK):
+            for at, qt in enumerate(qts):
                 for c in range(ncb):
                     u = qt * ncb + c
                     nc.tensor.matmul_mx(
-                        out=pv[:, qt * D:(qt + 1) * D],
+                        out=pv[:, at * D:(at + 1) * D],
                         lhsT=blocks[g]["codes"][:, u * P:(u + 1) * P].bitcast(FP8X4),
                         lhsT_scale=blocks[g]["scl"][:, u * P:(u + 1) * P],
                         rhs=vcs[h][:, (lo + c) * D:(lo + c + 1) * D].bitcast(FP8X4),
@@ -241,36 +267,51 @@ def tile_blocksparseattention_t_kernel(tc, q, k, v, out):
                         stop=(c == ncb - 1),
                     )
 
-        def sums(g):
-            rinv = small.tile([P, PACK], F32, name="rinv", tag="rinv")
-            nc.vector.reciprocal(out=rinv[:], in_=blocks[g]["rs"][:])
-            blocks[g]["rinv"] = rinv
+        def sums(g, q0, q1):
+            if q0 == 0:
+                blocks[g]["rinv"] = small.tile([P, PACK], F32, name="rinv", tag="rinv")
+            nc.vector.reciprocal(out=blocks[g]["rinv"][:, q0:q1], in_=blocks[g]["rs"][:, q0:q1])
 
-        def finish(g):
+        def finish(g, q0, q1, pv):
             h, i = divmod(g, NBLK)
+            w = (q1 - q0) * D
             o_sb = work.tile([P, PACK * D], F32, name="o_sb", tag="o_sb")
             nc.vector.tensor_tensor(
-                out=o_sb[:].rearrange("p (a d) -> p a d", a=PACK),
-                in0=blocks[g]["pv"][:].rearrange("p (a d) -> p a d", a=PACK),
-                in1=blocks[g]["rinv"][:].unsqueeze(2).to_broadcast([P, PACK, D]),
+                out=o_sb[:, 0:w].rearrange("p (a d) -> p a d", d=D),
+                in0=pv[:, 0:w].rearrange("p (a d) -> p a d", d=D),
+                in1=blocks[g]["rinv"][:, q0:q1].unsqueeze(2).to_broadcast([P, q1 - q0, D]),
                 op=ALU.mult,
             )
             nc.sync.dma_start(
-                out=out[0, h, i * BLK:(i + 1) * BLK, :].rearrange("(p t) d -> p (t d)", t=PACK),
-                in_=o_sb[:],
+                out=out[0, h, i * BLK:(i + 1) * BLK, :].rearrange("(p t) d -> p (t d)", t=PACK)[:, q0 * D:q1 * D],
+                in_=o_sb[:, 0:w],
             )
 
-        load(0)
+        new_raws(0)
+        load_k(0, 0, 1)
+        load_rows(0, 1, q, 0, 1, nc.scalar)
+        load_k(0, 1, 1)
+        load_rows(0, 1, q, 1, 1, nc.scalar)
+        load_rows(0, 2, v, 0, 2, nc.sync)
         load(1)
-        prep_first(0)
-        prep_second(0)
-        prep_first(1)
-        prep_second(1)
+        new_head(0)
+
+        def part_prep(g, at, eng_copy):
+            tp = ps_t.tile([P, 2 * BLK], BF16, name="tp", tag="tp")
+            if at == 0:
+                turn_k(g, tp)
+            else:
+                turn_q(g, tp, 0)
+            eng_copy(out=kqs[0][:, g, at:at + BLK].bitcast(F32), in_=tp[:, 0:BLK].bitcast(F32))
+
+        part_prep(0, 0, nc.scalar.copy)
+        part_prep(0, BLK, nc.vector.tensor_copy)
+        part_prep(1, 0, nc.scalar.copy)
 
         GL = (LT + 3) // PACK + 1
         turned = {}
         copied = {}
-        for it in range(ntiles + PACK * GL + PACK):
+        for it in range(ntiles + LT - 1):
             g4, r4 = divmod(it, PACK)
             if r4 == 0 and g4 % 2 == 0 and g4 // 2 + 2 < total // 2:
                 load(g4 // 2 + 2)
@@ -278,30 +319,63 @@ def tile_blocksparseattention_t_kernel(tc, q, k, v, out):
             for c in range(3):
                 if it < ntiles and c < span(it // PACK)[1]:
                     scores(it, c)
-                if 0 <= it - LT < ntiles and c < span((it - LT) // PACK)[1]:
+                if 0 <= it - LT and c < span((it - LT) // PACK)[1]:
                     turn(it - LT, c, done)
-            turned[it] = choose(done, it >= ntiles + TAIL_V)
+            if it == 0:
+                part_prep(1, BLK, nc.scalar.copy)
+            banks = []
+            for bank in done:
+                cnt = state["copies"]
+                state["copies"] = cnt + 1
+                if it >= ntiles - CATCH_UP:
+                    banks.append((bank, it < ntiles + 2))
+                else:
+                    banks.append((bank, cnt % VEC_OF == VEC_OF - 1))
             if 0 <= it - 2 < ntiles:
                 exps(it - 2)
             got = []
-            for bank, on_vector in turned.get(it, []):
+            for bank, on_vector in banks:
                 if not on_vector:
                     got.append(copy_out(bank, False))
             if r4 == 1 and g4 + 2 < total:
                 prep_second(g4 + 2)
-            for item in copied.get(it - 1, []):
-                quantise(item)
-            for bank, on_vector in turned.get(it, []):
+            for g, u0, grp in copied.get(it - 1, []):
+                quantise_units(g, u0, u0 + 2, grp[:])
+            if r4 == 3 and g4 < total:
+                v_second(g4)
+            for bank, on_vector in banks:
                 if on_vector:
                     got.append(copy_out(bank, True))
             copied[it] = got
             if it < ntiles:
                 shift(it)
-            if r4 == 3 and 0 <= g4 - GL < total:
-                finish(g4 - GL)
-            if r4 == 2 and 0 <= g4 - 1 < total:
-                sums(g4 - 1)
-            if r4 == 2 and 0 <= g4 - GL < total:
-                weighted(g4 - GL)
+            if r4 == 2 and 0 <= g4 - 1 < total - 1:
+                sums(g4 - 1, 0, PACK)
+            if r4 == 2 and 0 <= g4 - GL:
+                finish(g4 - GL, 0, PACK, blocks[g4 - GL]["pv"])
+            if r4 == 1 and 0 <= g4 - GL:
+                blocks[g4 - GL]["pv"] = ps_o.tile([P, PACK * D], F32, name="pv", tag="pv")
+                weighted(g4 - GL, range(PACK), blocks[g4 - GL]["pv"])
+            if r4 == 0 and g4 < total:
+                v_first(g4)
             if r4 == 0 and g4 + 2 < total:
                 prep_first(g4 + 2)
+
+        gl = total - 1
+        u0 = 3 * 2
+        grp = work.tile([P, 2 * BLK], BF16, name="grp", tag="grp", bufs=6, align_bytes=64)
+        for c, eng_copy in enumerate((nc.vector.tensor_copy, nc.scalar.copy)):
+            tp = ps_t.tile([P, BLK], F32, name="tp", tag="tp")
+            turn_chunk(last, c, tp, 0)
+            copy_words(eng_copy, grp[:, c * BLK:(c + 1) * BLK], tp[:, 0:HW], 1)
+        quantise_units(gl, u0, u0 + 1, grp[:, 0:BLK])
+        sums(gl, 0, PACK)
+        for g, i0, early in copied[ntiles + LT - 2]:
+            quantise_units(g, i0, i0 + 2, early[:])
+        quantise_units(gl, u0 + 1, u0 + 2, grp[:, BLK:2 * BLK])
+        pv = ps_o.tile([P, PACK * D], F32, name="pv", tag="pv")
+        weighted(gl, range(3), pv)
+        finish(gl, 0, 3, pv)
+        pv = ps_s.tile([P, BLK], F32, name="sp", tag="sp")
+        weighted(gl, (3,), pv)
+        finish(gl, 3, 4, pv)

@@ -25,7 +25,6 @@ SCALE = 1.0 / math.sqrt(D)
 
 VEC_OF = 16
 LT = 4
-CATCH_UP = 3
 HW = BLK // 2
 
 
@@ -321,23 +320,20 @@ def tile_blocksparseattention_t_kernel(tc, q, k, v, out):
                     scores(it, c)
                 if 0 <= it - LT and c < span((it - LT) // PACK)[1]:
                     turn(it - LT, c, done)
-            if it == 0:
+            if it == 1:
                 part_prep(1, BLK, nc.scalar.copy)
             banks = []
             for bank in done:
                 cnt = state["copies"]
                 state["copies"] = cnt + 1
-                if it >= ntiles - CATCH_UP:
-                    banks.append((bank, it < ntiles + 2))
-                else:
-                    banks.append((bank, cnt % VEC_OF == VEC_OF - 1))
+                banks.append((bank, ntiles <= it < ntiles + 2 or cnt % VEC_OF == VEC_OF - 1))
             if 0 <= it - 2 < ntiles:
                 exps(it - 2)
             got = []
             for bank, on_vector in banks:
                 if not on_vector:
                     got.append(copy_out(bank, False))
-            if r4 == 1 and g4 + 2 < total:
+            if it == 3 or r4 == 1 and 2 < g4 + 2 < total:
                 prep_second(g4 + 2)
             for g, u0, grp in copied.get(it - 1, []):
                 quantise_units(g, u0, u0 + 2, grp[:])
@@ -358,7 +354,7 @@ def tile_blocksparseattention_t_kernel(tc, q, k, v, out):
                 weighted(g4 - GL, range(PACK), blocks[g4 - GL]["pv"])
             if r4 == 0 and g4 < total:
                 v_first(g4)
-            if r4 == 0 and g4 + 2 < total:
+            if it == 2 or r4 == 0 and 2 < g4 + 2 < total:
                 prep_first(g4 + 2)
 
         gl = total - 1

@@ -23,7 +23,7 @@ PAIRS = H * (3 * NBLK - 2)
 FLOPS = 2 * 2 * PAIRS * BLK * BLK * D
 SCALE = 1.0 / math.sqrt(D)
 
-VEC_OF = 16
+VEC_OF = 14
 LT = 4
 HW = BLK // 2
 
@@ -45,6 +45,9 @@ def tile_blocksparseattention_t_kernel(tc, q, k, v, out):
         identf = const.tile([P, P], F32, name="identf")
         make_identity(nc, identf[:])
 
+        minus1 = const.tile([P, PACK], F32, name="minus1")
+        nc.gpsimd.memset(minus1[:], -1.0)
+
         ctx.enter_context(tc.manual_schedule())
 
         total = H * NBLK
@@ -58,7 +61,7 @@ def tile_blocksparseattention_t_kernel(tc, q, k, v, out):
         vgs = {}
         blocks = {}
         tiles = {}
-        state = {"copies": 0, "tp": None}
+        state = {"copies": 0, "tp": None, "grp": None}
 
         def span(g):
             i = g % NBLK
@@ -113,11 +116,11 @@ def tile_blocksparseattention_t_kernel(tc, q, k, v, out):
                         identity=ident[:],
                     )
 
-        def turn_q(g, tp, at):
+        def turn_q(g, tp, at, t0=0, t1=PACK):
             qraw = raws[g // 2][1]
-            for t in range(PACK):
+            for t in range(t0, t1):
                 nc.tensor.transpose(
-                    out=tp[:, at + t * P:at + (t + 1) * P],
+                    out=tp[:, at + (t - t0) * P:at + (t + 1 - t0) * P],
                     in_=qraw[:, g % 2, t * D:(t + 1) * D],
                     identity=ident[:],
                 )
@@ -225,8 +228,10 @@ def tile_blocksparseattention_t_kernel(tc, q, k, v, out):
             if u % 2 == 0:
                 state["tp"] = ps_t.tile([P, BLK], F32, name="tp", tag="tp")
             turn_chunk(n, c, state["tp"], (u % 2) * HW)
+            if u % 4 == 0:
+                state["grp"] = work.tile([P, 4 * BLK], BF16, name="grp", tag="grp", bufs=4, align_bytes=64)
             if u % 2 == 1:
-                done.append((g, u - 1, state["tp"]))
+                done.append((g, u - 1, state["tp"], state["grp"]))
 
         def copy_words(eng_copy, grp, tp, a):
             eng_copy(
@@ -235,10 +240,14 @@ def tile_blocksparseattention_t_kernel(tc, q, k, v, out):
             )
 
         def copy_out(bank, on_vector):
-            g, u0, tp = bank
-            grp = work.tile([P, 2 * BLK], BF16, name="grp", tag="grp", bufs=6, align_bytes=64)
-            copy_words(nc.vector.tensor_copy if on_vector else nc.scalar.copy, grp[:], tp[:], 2)
-            return (g, u0, grp)
+            g, u0, tp, grp = bank
+            half = grp[:, (u0 % 4) * BLK:(u0 % 4 + 2) * BLK]
+            copy_words(nc.vector.tensor_copy if on_vector else nc.scalar.copy, half, tp[:], 2)
+            if u0 % 4 == 2:
+                return [(g, u0 - 2, u0 + 2, grp[:])]
+            if g == total - 1 and u0 == 4:
+                return [(g, u0, u0 + 2, half)]
+            return []
 
         def quantise_units(g, u0, u1, src):
             if u0 == 0:
@@ -269,7 +278,9 @@ def tile_blocksparseattention_t_kernel(tc, q, k, v, out):
         def sums(g, q0, q1):
             if q0 == 0:
                 blocks[g]["rinv"] = small.tile([P, PACK], F32, name="rinv", tag="rinv")
-            nc.vector.reciprocal(out=blocks[g]["rinv"][:, q0:q1], in_=blocks[g]["rs"][:, q0:q1])
+            nc.gpsimd.tensor_tensor(
+                out=blocks[g]["rinv"][:, q0:q1], in0=blocks[g]["rs"][:, q0:q1], in1=minus1[:, q0:q1], op=ALU.pow,
+            )
 
         def finish(g, q0, q1, pv):
             h, i = divmod(g, NBLK)
@@ -288,24 +299,35 @@ def tile_blocksparseattention_t_kernel(tc, q, k, v, out):
 
         new_raws(0)
         load_k(0, 0, 1)
-        load_rows(0, 1, q, 0, 1, nc.scalar)
+        q0 = q[0, 0, 0:BLK, :].rearrange("(p t) d -> p (t d)", t=PACK)
+        nc.scalar.dma_start(out=raws[0][1][:, 0, 0:D], in_=q0[:, 0:D])
         load_k(0, 1, 1)
+        nc.scalar.dma_start(out=raws[0][1][:, 0, D:PACK * D], in_=q0[:, D:PACK * D])
         load_rows(0, 1, q, 1, 1, nc.scalar)
+        new_raws(1)
+        load_k(1, 0, 1)
+        load_rows(1, 1, q, 0, 1, nc.sync)
         load_rows(0, 2, v, 0, 2, nc.sync)
-        load(1)
+        load_k(1, 1, 1)
+        load_rows(1, 1, q, 1, 1, nc.sync)
+        load_rows(1, 2, v, 0, 2, nc.sync)
         new_head(0)
 
-        def part_prep(g, at, eng_copy):
+        def prep_k(g):
             tp = ps_t.tile([P, 2 * BLK], BF16, name="tp", tag="tp")
-            if at == 0:
-                turn_k(g, tp)
-            else:
-                turn_q(g, tp, 0)
-            eng_copy(out=kqs[0][:, g, at:at + BLK].bitcast(F32), in_=tp[:, 0:BLK].bitcast(F32))
+            turn_k(g, tp)
+            nc.scalar.copy(out=kqs[0][:, g, 0:BLK].bitcast(F32), in_=tp[:, 0:BLK].bitcast(F32))
 
-        part_prep(0, 0, nc.scalar.copy)
-        part_prep(0, BLK, nc.vector.tensor_copy)
-        part_prep(1, 0, nc.scalar.copy)
+        def prep_q(g, t0, t1, eng_copy):
+            tp = ps_t.tile([P, 2 * BLK], BF16, name="tp", tag="tp")
+            turn_q(g, tp, 0, t0, t1)
+            w = (t1 - t0) * P
+            at = BLK + t0 * P
+            eng_copy(out=kqs[0][:, g, at:at + w].bitcast(F32), in_=tp[:, 0:w].bitcast(F32))
+
+        prep_k(0)
+        prep_q(0, 0, 1, nc.vector.tensor_copy)
+        prep_k(1)
 
         GL = (LT + 3) // PACK + 1
         turned = {}
@@ -318,10 +340,12 @@ def tile_blocksparseattention_t_kernel(tc, q, k, v, out):
             for c in range(3):
                 if it < ntiles and c < span(it // PACK)[1]:
                     scores(it, c)
+                    if it == 0 and c == 0:
+                        prep_q(0, 1, PACK, nc.scalar.copy)
                 if 0 <= it - LT and c < span((it - LT) // PACK)[1]:
                     turn(it - LT, c, done)
-            if it == 1:
-                part_prep(1, BLK, nc.scalar.copy)
+            if it == 3:
+                prep_first(2)
             banks = []
             for bank in done:
                 cnt = state["copies"]
@@ -329,19 +353,21 @@ def tile_blocksparseattention_t_kernel(tc, q, k, v, out):
                 banks.append((bank, ntiles <= it < ntiles + 2 or cnt % VEC_OF == VEC_OF - 1))
             if 0 <= it - 2 < ntiles:
                 exps(it - 2)
+            if it == 2:
+                prep_q(1, 0, PACK, nc.scalar.copy)
             got = []
             for bank, on_vector in banks:
                 if not on_vector:
-                    got.append(copy_out(bank, False))
+                    got.extend(copy_out(bank, False))
             if it == 3 or r4 == 1 and 2 < g4 + 2 < total:
                 prep_second(g4 + 2)
-            for g, u0, grp in copied.get(it - 1, []):
-                quantise_units(g, u0, u0 + 2, grp[:])
+            for item in copied.get(it - 1, []):
+                quantise_units(*item)
             if r4 == 3 and g4 < total:
                 v_second(g4)
             for bank, on_vector in banks:
                 if on_vector:
-                    got.append(copy_out(bank, True))
+                    got.extend(copy_out(bank, True))
             copied[it] = got
             if it < ntiles:
                 shift(it)
@@ -352,26 +378,26 @@ def tile_blocksparseattention_t_kernel(tc, q, k, v, out):
             if r4 == 1 and 0 <= g4 - GL:
                 blocks[g4 - GL]["pv"] = ps_o.tile([P, PACK * D], F32, name="pv", tag="pv")
                 weighted(g4 - GL, range(PACK), blocks[g4 - GL]["pv"])
-            if r4 == 0 and g4 < total:
+            if r4 == 1 and g4 < total:
                 v_first(g4)
-            if it == 2 or r4 == 0 and 2 < g4 + 2 < total:
+            if r4 == 0 and 2 < g4 + 2 < total:
                 prep_first(g4 + 2)
 
         gl = total - 1
         u0 = 3 * 2
-        grp = work.tile([P, 2 * BLK], BF16, name="grp", tag="grp", bufs=6, align_bytes=64)
+        grp = work.tile([P, 4 * BLK], BF16, name="grp", tag="grp", bufs=4, align_bytes=64)
         for c, eng_copy in enumerate((nc.vector.tensor_copy, nc.scalar.copy)):
             tp = ps_t.tile([P, BLK], F32, name="tp", tag="tp")
             turn_chunk(last, c, tp, 0)
             copy_words(eng_copy, grp[:, c * BLK:(c + 1) * BLK], tp[:, 0:HW], 1)
         quantise_units(gl, u0, u0 + 1, grp[:, 0:BLK])
         sums(gl, 0, PACK)
-        for g, i0, early in copied[ntiles + LT - 2]:
-            quantise_units(g, i0, i0 + 2, early[:])
-        quantise_units(gl, u0 + 1, u0 + 2, grp[:, BLK:2 * BLK])
         pv = ps_o.tile([P, PACK * D], F32, name="pv", tag="pv")
-        weighted(gl, range(3), pv)
-        finish(gl, 0, 3, pv)
+        weighted(gl, (0, 1), pv)
+        for item in copied[ntiles + LT - 2]:
+            quantise_units(*item)
+        quantise_units(gl, u0 + 1, u0 + 2, grp[:, BLK:2 * BLK])
+        finish(gl, 0, 2, pv)
         pv = ps_s.tile([P, BLK], F32, name="sp", tag="sp")
-        weighted(gl, (3,), pv)
-        finish(gl, 3, 4, pv)
+        weighted(gl, (2, 3), pv)
+        finish(gl, 2, 4, pv)

@@ -23,7 +23,7 @@ PAIRS = H * (3 * NBLK - 2)
 FLOPS = 2 * 2 * PAIRS * BLK * BLK * D
 SCALE = 1.0 / math.sqrt(D)
 
-VEC_OF = 14
+VEC_OF = 20
 LT = 4
 HW = BLK // 2
 

@@ -23,7 +23,6 @@ PAIRS = H * (3 * NBLK - 2)
 FLOPS = 2 * 2 * PAIRS * BLK * BLK * D
 SCALE = 1.0 / math.sqrt(D)
 
-VEC_OF = 20
 LT = 4
 HW = BLK // 2
 
@@ -61,7 +60,7 @@ def tile_blocksparseattention_t_kernel(tc, q, k, v, out):
         vgs = {}
         blocks = {}
         tiles = {}
-        state = {"copies": 0, "tp": None, "grp": None}
+        state = {"tp": None, "grp": None}
 
         def span(g):
             i = g % NBLK
@@ -134,7 +133,8 @@ def tile_blocksparseattention_t_kernel(tc, q, k, v, out):
 
         def prep_second(g):
             h, b = divmod(g, NBLK)
-            nc.scalar.copy(out=kqs[h][:, b, :].bitcast(F32), in_=preps[g][:].bitcast(F32))
+            eng_copy = nc.vector.tensor_copy if b % 3 == 1 else nc.scalar.copy
+            eng_copy(out=kqs[h][:, b, :].bitcast(F32), in_=preps[g][:].bitcast(F32))
 
         def v_first(g):
             vg = work.tile([P, BLK], BF16, name="vg", tag="vg", align_bytes=64)
@@ -346,11 +346,7 @@ def tile_blocksparseattention_t_kernel(tc, q, k, v, out):
                     turn(it - LT, c, done)
             if it == 3:
                 prep_first(2)
-            banks = []
-            for bank in done:
-                cnt = state["copies"]
-                state["copies"] = cnt + 1
-                banks.append((bank, ntiles <= it < ntiles + 2 or cnt % VEC_OF == VEC_OF - 1))
+            banks = [(bank, ntiles <= it < ntiles + 2) for bank in done]
             if 0 <= it - 2 < ntiles:
                 exps(it - 2)
             if it == 2:

from contextlib import ExitStack
import math

import concourse.mybir as mybir
from concourse.masks import make_identity

F32 = mybir.dt.float32
BF16 = mybir.dt.bfloat16
U32 = mybir.dt.uint32
U8 = mybir.dt.uint8
FP8X4 = mybir.dt.float8_e4m3fn_x4
ALU = mybir.AluOpType
ACT = mybir.ActivationFunctionType

H = 4
S = 4096
D = 128
P = 128
BLK = 512
NBLK = S // BLK
PACK = 4
PAIRS = H * (3 * NBLK - 2)
FLOPS = 2 * 2 * PAIRS * BLK * BLK * D
SCALE = 1.0 / math.sqrt(D)

LT = 4
HW = BLK // 2


def tile_blocksparseattention_t_kernel(tc, q, k, v, out):
    nc = tc.nc
    with ExitStack() as ctx:
        const = ctx.enter_context(tc.tile_pool(name="const", bufs=1))
        raw = ctx.enter_context(tc.tile_pool(name="raw", bufs=3))
        heads = ctx.enter_context(tc.tile_pool(name="heads", bufs=2))
        work = ctx.enter_context(tc.tile_pool(name="work", bufs=3))
        small = ctx.enter_context(tc.tile_pool(name="small", bufs=4))
        ps_s = ctx.enter_context(tc.psum_pool(name="ps_s", bufs=3))
        ps_t = ctx.enter_context(tc.psum_pool(name="ps_t", bufs=4))
        ps_o = ctx.enter_context(tc.psum_pool(name="ps_o", bufs=1))

        ident = const.tile([P, P], BF16, name="ident")
        make_identity(nc, ident[:])
        identf = const.tile([P, P], F32, name="identf")
        make_identity(nc, identf[:])

        minus1 = const.tile([P, PACK], F32, name="minus1")
        nc.gpsimd.memset(minus1[:], -1.0)

        ctx.enter_context(tc.manual_schedule())

        total = H * NBLK
        ntiles = total * PACK
        last = ntiles - 1
        raws = {}
        kqs = {}
        vcs = {}
        vss = {}
        preps = {}
        vgs = {}
        blocks = {}
        tiles = {}
        state = {"tp": None, "grp": None}

        def span(g):
            i = g % NBLK
            lo = max(i - 1, 0)
            return lo, min(i + 2, NBLK) - lo

        def load_k(pair, b0, nb):
            h, b2 = divmod(pair, NBLK // 2)
            r0 = (b2 * 2 + b0) * BLK
            kraw = raws[pair][0]
            for u in range(2):
                for e in range(2):
                    nc.sync.dma_start(
                        out=kraw[e:P:2, 2 * b0:2 * (b0 + nb), u, :],
                        in_=k[0, h, r0 + 2 * u + e:r0 + nb * BLK:4, :].rearrange("(a j) d -> j a d", j=P // 2),
                    )

        def load_rows(pair, which, src, b0, nb, eng):
            h, b2 = divmod(pair, NBLK // 2)
            r0 = (b2 * 2 + b0) * BLK
            eng.dma_start(
                out=raws[pair][which][:, b0:b0 + nb, :],
                in_=src[0, h, r0:r0 + nb * BLK, :].rearrange("(b p t) d -> p b (t d)", b=nb, p=P, t=PACK),
            )

        def new_raws(pair):
            kraw = raw.tile([P, 4, 2, D], BF16, name="kraw", tag="kraw")
            qraw = raw.tile([P, 2, BLK], BF16, name="qraw", tag="qraw")
            vraw = raw.tile([P, 2, BLK], BF16, name="vraw", tag="vraw")
            raws[pair] = (kraw, qraw, vraw)

        def load(pair):
            new_raws(pair)
            load_k(pair, 0, 2)
            load_rows(pair, 1, q, 0, 2, nc.sync)
            load_rows(pair, 2, v, 0, 2, nc.sync)

        def new_head(g):
            h, b = divmod(g, NBLK)
            if b == 0:
                kqs[h] = heads.tile([P, NBLK, 2 * BLK], BF16, name="kq", tag="kq")
                vcs[h] = heads.tile([P, NBLK * D], U32, name="vcodes", tag="vcodes", align_bytes=64)
                vss[h] = heads.tile([P, NBLK * D], U8, name="vscales", tag="vscales", align_bytes=64)

        def turn_k(g, tp):
            kraw = raws[g // 2][0]
            for u in range(2):
                for a in range(2):
                    nc.tensor.transpose(
                        out=tp[:, u * HW + a * P:u * HW + (a + 1) * P],
                        in_=kraw[:, (g % 2) * 2 + a, u, :],
                        identity=ident[:],
                    )

        def turn_q(g, tp, at, t0=0, t1=PACK):
            qraw = raws[g // 2][1]
            for t in range(t0, t1):
                nc.tensor.transpose(
                    out=tp[:, at + (t - t0) * P:at + (t + 1 - t0) * P],
                    in_=qraw[:, g % 2, t * D:(t + 1) * D],
                    identity=ident[:],
                )

        def prep_first(g):
            new_head(g)
            tp = ps_t.tile([P, 2 * BLK], BF16, name="tp", tag="tp")
            turn_k(g, tp)
            turn_q(g, tp, BLK)
            preps[g] = tp

        def prep_second(g):
            h, b = divmod(g, NBLK)
            eng_copy = nc.vector.tensor_copy if b % 3 == 1 else nc.scalar.copy
            eng_copy(out=kqs[h][:, b, :].bitcast(F32), in_=preps[g][:].bitcast(F32))

        def v_first(g):
            vg = work.tile([P, BLK], BF16, name="vg", tag="vg", align_bytes=64)
            nc.gpsimd.tensor_copy(
                out=vg[:].rearrange("p (c i t) -> p c t i", i=4, t=PACK),
                in_=raws[g // 2][2][:, g % 2, :].rearrange("p (t c i) -> p c t i", t=PACK, i=4),
            )
            vgs[g] = vg

        def v_second(g):
            h, b = divmod(g, NBLK)
            nc.vector.quantize_mx(
                out=vcs[h][:, b * D:(b + 1) * D].bitcast(FP8X4),
                scales=vss[h][:, b * D:(b + 1) * D],
                in_=vgs[g][:],
            )

        def scores(n, c):
            g, qt = divmod(n, PACK)
            h, i = divmod(g, NBLK)
            lo, ncb = span(g)
            if c == 0:
                tiles[n] = {
                    "mx": small.tile([P, 4], F32, name="mx", tag="mx"),
                    "ssb": work.tile([P, 3 * BLK], F32, name="ssb", tag="ssb", bufs=4),
                }
            sp = ps_s.tile([P, BLK], F32, name="sp", tag="sp")
            nc.tensor.matmul(
                out=sp[:],
                lhsT=kqs[h][:, i, BLK + qt * P:BLK + (qt + 1) * P],
                rhs=kqs[h][:, lo + c, 0:BLK],
                start=True,
                stop=True,
            )
            nc.vector.tensor_scalar(
                out=tiles[n]["ssb"][:, c * BLK:(c + 1) * BLK], in0=sp[:], scalar1=-SCALE, scalar2=None,
                op0=ALU.mult, op1=ALU.min, accum_out=tiles[n]["mx"][:, c:c + 1],
            )

        def shift(n):
            ncb = span(n // PACK)[1]
            mx = tiles[n]["mx"]
            negm = small.tile([P, 1], F32, name="negm", tag="negm")
            if ncb == 2:
                nc.gpsimd.tensor_scalar(
                    out=negm[:], in0=mx[:, 0:1], scalar1=mx[:, 1:2], scalar2=None, op0=ALU.min,
                )
            else:
                nc.gpsimd.tensor_scalar(
                    out=negm[:], in0=mx[:, 0:1], scalar1=mx[:, 1:2], scalar2=mx[:, 2:3],
                    op0=ALU.min, op1=ALU.min,
                )
            tiles[n]["negm"] = negm

        def exp(n, c0, c1, total_out):
            nc.scalar.activation(
                out=tiles[n]["e"][:, c0 * BLK:c1 * BLK],
                in_=tiles[n]["ssb"][:, c0 * BLK:c1 * BLK],
                func=ACT.Exp, bias=tiles[n]["negm"][:, 0:1], scale=-1.0,
                accum_out=total_out,
            )

        def exps(n):
            g, qt = divmod(n, PACK)
            ncb = span(g)[1]
            if qt == 0:
                blocks[g] = {"rs": small.tile([P, PACK], F32, name="rs", tag="rs")}
            tiles[n]["e"] = work.tile([P, 3 * BLK], BF16, name="e", tag="e", bufs=LT)
            if n < last:
                exp(n, 0, ncb, blocks[g]["rs"][:, qt:qt + 1])
            else:
                parts = small.tile([P, 2], F32, name="parts", tag="parts")
                exp(n, 0, 1, parts[:, 0:1])
                exp(n, 1, 2, parts[:, 1:2])
                nc.gpsimd.tensor_tensor(
                    out=blocks[g]["rs"][:, qt:qt + 1], in0=parts[:, 0:1], in1=parts[:, 1:2], op=ALU.add,
                )

        def turn_chunk(n, c, tp, at):
            words = tiles[n]["e"][:].bitcast(F32)
            for w in range(2):
                nc.tensor.transpose(
                    out=tp[:, at + w * P:at + (w + 1) * P],
                    in_=words[:, c * HW + w * P:c * HW + (w + 1) * P],
                    identity=identf[:],
                )

        def turn(n, c, done):
            g, qt = divmod(n, PACK)
            u = qt * span(g)[1] + c
            if u % 2 == 0:
                state["tp"] = ps_t.tile([P, BLK], F32, name="tp", tag="tp")
            turn_chunk(n, c, state["tp"], (u % 2) * HW)
            if u % 4 == 0:
                state["grp"] = work.tile([P, 4 * BLK], BF16, name="grp", tag="grp", bufs=4, align_bytes=64)
            if u % 2 == 1:
                done.append((g, u - 1, state["tp"], state["grp"]))

        def copy_words(eng_copy, grp, tp, a):
            eng_copy(
                out=grp.bitcast(F32).rearrange("p (a q w) -> p a q w", a=a, w=2),
                in_=tp.rearrange("p (a w q) -> p a q w", a=a, w=2),
            )

        def copy_out(bank, on_vector):
            g, u0, tp, grp = bank
            half = grp[:, (u0 % 4) * BLK:(u0 % 4 + 2) * BLK]
            copy_words(nc.vector.tensor_copy if on_vector else nc.scalar.copy, half, tp[:], 2)
            if u0 % 4 == 2:
                return [(g, u0 - 2, u0 + 2, grp[:])]
            if g == total - 1 and u0 == 4:
                return [(g, u0, u0 + 2, half)]
            return []

        def quantise_units(g, u0, u1, src):
            if u0 == 0:
                blocks[g]["codes"] = work.tile([P, PACK * 3 * P], U32, name="codes", tag="codes", align_bytes=64)
                blocks[g]["scl"] = work.tile([P, PACK * 3 * P], U8, name="scl", tag="scl", align_bytes=64)
            nc.vector.quantize_mx(
                out=blocks[g]["codes"][:, u0 * P:u1 * P].bitcast(FP8X4),
                scales=blocks[g]["scl"][:, u0 * P:u1 * P],
                in_=src,
            )

        def weighted(g, qts, pv):
            h = g // NBLK
            lo, ncb = span(g)
            for at, qt in enumerate(qts):
                for c in range(ncb):
                    u = qt * ncb + c
                    nc.tensor.matmul_mx(
                        out=pv[:, at * D:(at + 1) * D],
                        lhsT=blocks[g]["codes"][:, u * P:(u + 1) * P].bitcast(FP8X4),
                        lhsT_scale=blocks[g]["scl"][:, u * P:(u + 1) * P],
                        rhs=vcs[h][:, (lo + c) * D:(lo + c + 1) * D].bitcast(FP8X4),
                        rhs_scale=vss[h][:, (lo + c) * D:(lo + c + 1) * D],
                        start=(c == 0),
                        stop=(c == ncb - 1),
                    )

        def sums(g, q0, q1):
            if q0 == 0:
                blocks[g]["rinv"] = small.tile([P, PACK], F32, name="rinv", tag="rinv")
            nc.gpsimd.tensor_tensor(
                out=blocks[g]["rinv"][:, q0:q1], in0=blocks[g]["rs"][:, q0:q1], in1=minus1[:, q0:q1], op=ALU.pow,
            )

        def finish(g, q0, q1, pv):
            h, i = divmod(g, NBLK)
            w = (q1 - q0) * D
            o_sb = work.tile([P, PACK * D], F32, name="o_sb", tag="o_sb")
            nc.vector.tensor_tensor(
                out=o_sb[:, 0:w].rearrange("p (a d) -> p a d", d=D),
                in0=pv[:, 0:w].rearrange("p (a d) -> p a d", d=D),
                in1=blocks[g]["rinv"][:, q0:q1].unsqueeze(2).to_broadcast([P, q1 - q0, D]),
                op=ALU.mult,
            )
            nc.sync.dma_start(
                out=out[0, h, i * BLK:(i + 1) * BLK, :].rearrange("(p t) d -> p (t d)", t=PACK)[:, q0 * D:q1 * D],
                in_=o_sb[:, 0:w],
            )

        new_raws(0)
        load_k(0, 0, 1)
        q0 = q[0, 0, 0:BLK, :].rearrange("(p t) d -> p (t d)", t=PACK)
        nc.scalar.dma_start(out=raws[0][1][:, 0, 0:D], in_=q0[:, 0:D])
        load_k(0, 1, 1)
        nc.scalar.dma_start(out=raws[0][1][:, 0, D:PACK * D], in_=q0[:, D:PACK * D])
        load_rows(0, 1, q, 1, 1, nc.scalar)
        new_raws(1)
        load_k(1, 0, 1)
        load_rows(1, 1, q, 0, 1, nc.sync)
        load_rows(0, 2, v, 0, 2, nc.sync)
        load_k(1, 1, 1)
        load_rows(1, 1, q, 1, 1, nc.sync)
        load_rows(1, 2, v, 0, 2, nc.sync)
        new_head(0)

        def prep_k(g):
            tp = ps_t.tile([P, 2 * BLK], BF16, name="tp", tag="tp")
            turn_k(g, tp)
            nc.scalar.copy(out=kqs[0][:, g, 0:BLK].bitcast(F32), in_=tp[:, 0:BLK].bitcast(F32))

        def prep_q(g, t0, t1, eng_copy):
            tp = ps_t.tile([P, 2 * BLK], BF16, name="tp", tag="tp")
            turn_q(g, tp, 0, t0, t1)
            w = (t1 - t0) * P
            at = BLK + t0 * P
            eng_copy(out=kqs[0][:, g, at:at + w].bitcast(F32), in_=tp[:, 0:w].bitcast(F32))

        prep_k(0)
        prep_q(0, 0, 1, nc.vector.tensor_copy)
        prep_k(1)

        GL = (LT + 3) // PACK + 1
        turned = {}
        copied = {}
        for it in range(ntiles + LT - 1):
            g4, r4 = divmod(it, PACK)
            if r4 == 0 and g4 % 2 == 0 and g4 // 2 + 2 < total // 2:
                load(g4 // 2 + 2)
            done = []
            for c in range(3):
                if it < ntiles and c < span(it // PACK)[1]:
                    scores(it, c)
                    if it == 0 and c == 0:
                        prep_q(0, 1, PACK, nc.scalar.copy)
                if 0 <= it - LT and c < span((it - LT) // PACK)[1]:
                    turn(it - LT, c, done)
            if it == 3:
                prep_first(2)
            banks = [(bank, ntiles <= it < ntiles + 2) for bank in done]
            if 0 <= it - 2 < ntiles:
                exps(it - 2)
            if it == 2:
                prep_q(1, 0, PACK, nc.scalar.copy)
            got = []
            for bank, on_vector in banks:
                if not on_vector:
                    got.extend(copy_out(bank, False))
            if it == 3 or r4 == 1 and 2 < g4 + 2 < total:
                prep_second(g4 + 2)
            for item in copied.get(it - 1, []):
                quantise_units(*item)
            if r4 == 3 and g4 < total:
                v_second(g4)
            for bank, on_vector in banks:
                if on_vector:
                    got.extend(copy_out(bank, True))
            copied[it] = got
            if it < ntiles:
                shift(it)
            if r4 == 2 and 0 <= g4 - 1 < total - 1:
                sums(g4 - 1, 0, PACK)
            if r4 == 2 and 0 <= g4 - GL:
                finish(g4 - GL, 0, PACK, blocks[g4 - GL]["pv"])
            if r4 == 1 and 0 <= g4 - GL:
                blocks[g4 - GL]["pv"] = ps_o.tile([P, PACK * D], F32, name="pv", tag="pv")
                weighted(g4 - GL, range(PACK), blocks[g4 - GL]["pv"])
            if r4 == 1 and g4 < total:
                v_first(g4)
            if r4 == 0 and 2 < g4 + 2 < total:
                prep_first(g4 + 2)

        gl = total - 1
        u0 = 3 * 2
        grp = work.tile([P, 4 * BLK], BF16, name="grp", tag="grp", bufs=4, align_bytes=64)
        for c, eng_copy in enumerate((nc.vector.tensor_copy, nc.scalar.copy)):
            tp = ps_t.tile([P, BLK], F32, name="tp", tag="tp")
            turn_chunk(last, c, tp, 0)
            copy_words(eng_copy, grp[:, c * BLK:(c + 1) * BLK], tp[:, 0:HW], 1)
        quantise_units(gl, u0, u0 + 1, grp[:, 0:BLK])
        sums(gl, 0, PACK)
        pv = ps_o.tile([P, PACK * D], F32, name="pv", tag="pv")
        weighted(gl, (0, 1), pv)
        for item in copied[ntiles + LT - 2]:
            quantise_units(*item)
        quantise_units(gl, u0 + 1, u0 + 2, grp[:, BLK:2 * BLK])
        finish(gl, 0, 2, pv)
        pv = ps_s.tile([P, BLK], F32, name="sp", tag="sp")
        weighted(gl, (2, 3), pv)
        finish(gl, 2, 4, pv)
